import numpy as np
import ml_dtypes


def mxq(x, axis, fmt="e4m3"):
    dtype, down = {"e4m3": (ml_dtypes.float8_e4m3fn, 7), "e5m2": (ml_dtypes.float8_e5m2, 14)}[fmt]
    v = np.moveaxis(np.asarray(x, np.float32).astype(ml_dtypes.bfloat16).astype(np.float64), axis, -1)
    blocks = v.reshape(v.shape[:-1] + (-1, 32))
    amax = np.abs(blocks).max(-1, keepdims=True)
    byte = np.maximum(np.where(amax > 0, np.frexp(amax)[1] - 1 + 127, 0) - down, 1)
    scale = np.exp2(byte - 127.0)
    codes = (blocks / scale).astype(np.float32).astype(dtype).astype(np.float64)
    return np.moveaxis((codes * scale).reshape(v.shape), -1, axis)


WIDE = False


def mx_kscale(k):
    if not WIDE:
        return np.ones(k)
    levels = np.array([10, -10, 5, -5, 0])
    if k % 512:
        return np.exp2(np.random.permutation(np.resize(levels, k // 32))).repeat(32)
    a = np.empty((k // 512, 16))
    for p in range(k // 512):
        a[p, :8] = np.random.permutation(np.resize(levels, 8))
        for g in range(8):
            far = levels[np.abs(levels - a[p, g]) >= 10]
            a[p, g + 8] = far[np.random.randint(len(far))]
    return np.exp2(a.ravel()).repeat(32)


BF16 = ml_dtypes.bfloat16


def bf(x):
    return np.asarray(x, np.float32).astype(BF16)


def f64(x):
    return np.asarray(x).astype(np.float64)


B, N, C, H = 1, 1536, 2048, 1024
EPS = 1e-12


def layer_norm(v, w, b):
    u = v.mean(-1, keepdims=True)
    s = ((v - u) ** 2).mean(-1, keepdims=True)
    return w * ((v - u) / np.sqrt(s + EPS)) + b


def setup_inputs():
    s = mx_kscale(C)
    x = np.random.standard_normal((B, N, C)) * (0.4 + 1.2 * np.random.random((B, N)))[:, :, None] + 0.4 * np.random.standard_normal((B, N))[:, :, None]
    return {"x": bf(x),
            "pre_w": bf((1.0 + 0.1 * np.random.standard_normal(C)) * s),
            "pre_b": bf(0.2 * np.random.standard_normal(C) * s),
            "lin1_W": bf(np.random.standard_normal((H, C)) / np.sqrt(C) / s[None, :]),
            "lin1_b": bf(0.3 * np.random.standard_normal(H) + 0.3),
            "n1_w": bf(1.0 + 0.1 * np.random.standard_normal(H)),
            "n1_b": bf(0.2 * np.random.standard_normal(H))}


def reference(x, pre_w, pre_b, lin1_W, lin1_b, n1_w, n1_b):
    y = np.maximum(layer_norm(f64(x), f64(pre_w), f64(pre_b)), 0.0)
    y = (mxq(y, 2, "e4m3") @ mxq(f64(lin1_W), 1, "e4m3").T) + f64(lin1_b)
    return np.maximum(layer_norm(y, f64(n1_w), f64(n1_b)), 0.0)

@@ -1,0 +1,251 @@
+from contextlib import ExitStack
+
+import concourse.mybir as mybir
+from concourse.masks import make_identity
+
+F32 = mybir.dt.float32
+BF16 = mybir.dt.bfloat16
+I32 = mybir.dt.int32
+U32 = mybir.dt.uint32
+U8 = mybir.dt.uint8
+FP8X4 = mybir.dt.float8_e4m3fn_x4
+ACT = mybir.ActivationFunctionType
+ALU = mybir.AluOpType
+
+P = 128
+TOKENS = 1536
+C = 2048
+H = 1024
+EPS = 1e-12
+PACK = 4
+K_PASS = P * PACK
+PASSES = C // K_PASS
+BLOCKS = C // P
+TILES = TOKENS // P
+W_TILES = H // P
+GROUP = 4
+GROUP_TOKENS = GROUP * P
+N_COLS = 512
+HALVES = H // N_COLS
+BN_CHUNK = 512
+
+FLOPS = 2 * TOKENS * C * H
+
+
+def tile_graphresblock_pa_kernel(tc, x, pre_w, pre_b, lin1_W, lin1_b, n1_w, n1_b, out):
+    nc = tc.nc
+    x_rows = x.flatten_outer_dims()
+    out_rows = out.flatten_outer_dims()
+
+    with ExitStack() as stack:
+        const = stack.enter_context(tc.tile_pool(name="const", bufs=1))
+        small = stack.enter_context(tc.tile_pool(name="small", bufs=8))
+        rows_pool = stack.enter_context(tc.tile_pool(name="rows_pool", bufs=12))
+        xn_pool = stack.enter_context(tc.tile_pool(name="xn_pool", bufs=8))
+        stage = stack.enter_context(tc.tile_pool(name="stage", bufs=3))
+        y_pool = stack.enter_context(tc.tile_pool(name="y_pool", bufs=2))
+        z_pool = stack.enter_context(tc.tile_pool(name="z_pool", bufs=3))
+        psum_t = stack.enter_context(tc.psum_pool(name="psum_t", bufs=4))
+        psum_acc = stack.enter_context(tc.psum_pool(name="psum_acc", bufs=4))
+
+        ident = const.tile([P, P], F32)
+        make_identity(nc, ident[:])
+        eps_col = const.tile([P, 1], F32)
+        nc.vector.memset(eps_col[:], EPS)
+        table_warm = const.tile([P, 1], F32)
+        nc.scalar.activation(out=table_warm[:], in_=eps_col[:], func=ACT.Sqrt)
+        ones = const.tile([P, P], BF16)
+        nc.vector.memset(ones[:], 1.0)
+        wb_rows = const.tile([P, K_PASS], BF16)
+        nc.vector.memset(wb_rows[:].bitcast(I32), 0)
+        vec_rows = const.tile([P, 3, H], BF16)
+        nc.vector.memset(vec_rows[:].rearrange("p v h -> p (v h)").bitcast(I32), 0)
+
+        x_nat = {}
+        w_nat = {}
+
+        def load_x(n):
+            x_nat[n] = rows_pool.tile([P, C], BF16, name="x_nat", tag="rows")
+            nc.sync.dma_start(out=x_nat[n][:], in_=x_rows[P * n : P * n + P, :])
+
+        def load_w(r):
+            w_nat[r] = rows_pool.tile([P, C], BF16, name="w_nat", tag="rows")
+            nc.sync.dma_start(out=w_nat[r][:], in_=lin1_W[P * r : P * r + P, :])
+
+        for n in range(GROUP):
+            load_x(n)
+        nc.sync.dma_start(out=wb_rows[0:PASSES, :], in_=pre_w.rearrange("(a c) -> a c", c=K_PASS))
+        nc.sync.dma_start(out=wb_rows[PASSES : 2 * PASSES, :], in_=pre_b.rearrange("(a c) -> a c", c=K_PASS))
+        for r in range(W_TILES):
+            load_w(r)
+        for v, vec in enumerate((lin1_b, n1_w, n1_b)):
+            nc.sync.dma_start(out=vec_rows[0:1, v, :], in_=vec.rearrange("(o h) -> o h", o=1))
+        for n in range(GROUP, TILES):
+            load_x(n)
+
+        wb_t = psum_t.tile([P, 2, P], F32, tag="t")
+        for u in range(2):
+            nc.tensor.transpose(wb_t[:, u, :], wb_rows[:].bitcast(F32)[:, u : 2 * P : 2], ident[:])
+        wb_pairs = const.tile([P, 2 * BLOCKS], BF16)
+        nc.vector.tensor_copy(
+            out=wb_pairs[:].bitcast(F32).rearrange("p (a u) -> p a u", u=2),
+            in_=wb_t[:, :, 0 : 2 * PASSES].rearrange("p u a -> p a u"),
+        )
+        wb_cols = const.tile([P, 2 * BLOCKS], F32)
+        nc.vector.tensor_copy(out=wb_cols[:], in_=wb_pairs[:])
+
+        xn = {}
+
+        def normalise(n):
+            stats = small.tile([P, C // BN_CHUNK, 6], F32, name="stats")
+            for s in range(C // BN_CHUNK):
+                nc.vector.bn_stats(out=stats[:, s, :], in_=x_nat[n][:, BN_CHUNK * s : BN_CHUNK * (s + 1)])
+            mean_var = small.tile([P, 2], F32, name="mean_var")
+            nc.vector.bn_aggr(out=mean_var[:], in_=stats[:].rearrange("p s d -> p (s d)"))
+            std = small.tile([P, 1], F32, name="std")
+            nc.scalar.activation(out=std[:], in_=mean_var[:, 1:2], func=ACT.Sqrt, bias=eps_col[:], scale=1.0)
+            rstd = small.tile([P, 1], F32, name="rstd")
+            nc.vector.reciprocal(out=rstd[:], in_=std[:])
+            shift = small.tile([P, 1], F32, name="shift")
+            nc.vector.scalar_tensor_tensor(
+                out=shift[:], in0=mean_var[:, 0:1], scalar=-1.0, in1=rstd[:], op0=ALU.mult, op1=ALU.mult
+            )
+            xn[n] = xn_pool.tile([P, BLOCKS, P], F32, name="xn")
+            nc.scalar.activation(
+                out=xn[n][:].rearrange("p (g t) q -> p g t q", t=PACK),
+                in_=x_nat[n][:].rearrange("p (g q t) -> p g t q", q=P, t=PACK),
+                func=ACT.Identity,
+                scale=rstd[:],
+                bias=shift[:],
+            )
+
+        w_words = const.tile([P, PASSES, H], U32, align_bytes=64)
+        w_scales = const.tile([P, PASSES, H], U8, align_bytes=64)
+
+        def quantise_w(pair):
+            for g in range(PASSES):
+                wt = psum_t.tile([P, 2, 2 * P], F32, tag="t")
+                for u in range(2):
+                    for r in range(2):
+                        words = w_nat[2 * pair + r][:].bitcast(F32)
+                        first = 2 * P * g + u
+                        nc.tensor.transpose(
+                            wt[:, u, P * r : P * r + P], words[:, first : 2 * P * (g + 1) : 2], ident[:]
+                        )
+                w_grouped = stage.tile([P, 2 * P * PACK], BF16, align_bytes=64, name="w_grouped")
+                nc.scalar.copy(
+                    out=w_grouped[:].bitcast(F32).rearrange("p (h u) -> p h u", u=2),
+                    in_=wt[:].rearrange("p u h -> p h u"),
+                )
+                cols = slice(2 * P * pair, 2 * P * (pair + 1))
+                nc.vector.quantize_mx(
+                    out=w_words[:, g, cols].bitcast(FP8X4), scales=w_scales[:, g, cols], in_=w_grouped[:]
+                )
+
+        def spread(v):
+            spread_ps = psum_t.tile([P, H], BF16, tag="t")
+            for hh in range(HALVES):
+                cols = slice(N_COLS * hh, N_COLS * (hh + 1))
+                nc.tensor.matmul(out=spread_ps[:, cols], lhsT=ones[:], rhs=vec_rows[:, v, cols], start=True, stop=True)
+            spread_sb = const.tile([P, H], BF16, name="spread_sb%d" % v)
+            nc.scalar.copy(out=spread_sb[:], in_=spread_ps[:])
+            return spread_sb
+
+        y_words = {}
+        y_scales = {}
+
+        def quantise_y(group, g):
+            if g == 0:
+                y_words[group] = y_pool.tile([P, PASSES, GROUP_TOKENS], U32, align_bytes=64, name="y_words")
+                y_scales[group] = y_pool.tile([P, PASSES, GROUP_TOKENS], U8, align_bytes=64, name="y_scales")
+            y_planes = stage.tile([P, PACK, GROUP_TOKENS], BF16, name="y_planes")
+            for t in range(PACK):
+                j = PACK * g + t
+                xt = psum_t.tile([P, GROUP_TOKENS], F32, tag="t")
+                for i in range(GROUP):
+                    nc.tensor.transpose(xt[:, P * i : P * i + P], xn[GROUP * group + i][:, j, :], ident[:])
+                nc.scalar.activation(
+                    out=y_planes[:, t, :],
+                    in_=xt[:],
+                    func=ACT.Relu,
+                    scale=wb_cols[:, j : j + 1],
+                    bias=wb_cols[:, BLOCKS + j : BLOCKS + j + 1],
+                )
+            y_grouped = stage.tile([P, GROUP_TOKENS * PACK], BF16, align_bytes=64, name="y_grouped")
+            nc.vector.tensor_copy(
+                out=y_grouped[:].rearrange("p (c i t) -> p c t i", i=4, t=PACK),
+                in_=y_planes[:].rearrange("p t (c i) -> p c t i", i=4),
+            )
+            nc.vector.quantize_mx(
+                out=y_words[group][:, g, :].bitcast(FP8X4), scales=y_scales[group][:, g, :], in_=y_grouped[:]
+            )
+
+        def project(n):
+            group = n // GROUP
+            tok = slice(P * (n % GROUP), P * (n % GROUP) + P)
+            z = z_pool.tile([P, H], F32, name="z")
+            z_sum = small.tile([P, HALVES], F32, name="z_sum")
+            for hh in range(HALVES):
+                cols = slice(N_COLS * hh, N_COLS * (hh + 1))
+                acc = psum_acc.tile([P, N_COLS], F32, name="acc")
+                for g in range(PASSES):
+                    nc.tensor.matmul_mx(
+                        out=acc[:],
+                        lhsT=y_words[group][:, g, tok].bitcast(FP8X4),
+                        lhsT_scale=y_scales[group][:, g, tok],
+                        rhs=w_words[:, g, cols].bitcast(FP8X4),
+                        rhs_scale=w_scales[:, g, cols],
+                        start=(g == 0),
+                        stop=(g == PASSES - 1),
+                    )
+                nc.vector.scalar_tensor_tensor(
+                    out=z[:, cols],
+                    in0=acc[:],
+                    scalar=1.0,
+                    in1=bias_b[:, cols],
+                    op0=ALU.mult,
+                    op1=ALU.add,
+                    accum_out=z_sum[:, hh : hh + 1],
+                )
+            neg_mean = small.tile([P, 1], F32, name="neg_mean")
+            nc.vector.tensor_scalar(
+                out=neg_mean[:],
+                in0=z_sum[:, 0:1],
+                scalar1=z_sum[:, 1:2],
+                scalar2=-1.0 / H,
+                op0=ALU.add,
+                op1=ALU.mult,
+            )
+            squares = z_pool.tile([P, H], BF16, name="squares")
+            sum_sq = small.tile([P, 1], F32, name="sum_sq")
+            nc.scalar.activation(
+                out=squares[:], in_=z[:], func=ACT.Square, bias=neg_mean[:], scale=1.0, accum_out=sum_sq[:]
+            )
+            std2 = small.tile([P, 1], F32, name="std2")
+            nc.scalar.activation(out=std2[:], in_=sum_sq[:], func=ACT.Sqrt, bias=eps_col[:], scale=1.0 / H)
+            rstd2 = small.tile([P, 1], F32, name="rstd2")
+            nc.vector.reciprocal(out=rstd2[:], in_=std2[:])
+            res = z_pool.tile([P, H], F32, name="res")
+            nc.vector.scalar_tensor_tensor(
+                out=res[:], in0=z[:], scalar=neg_mean[:], in1=gain_b[:], op0=ALU.add, op1=ALU.mult
+            )
+            nc.vector.scalar_tensor_tensor(
+                out=res[:], in0=res[:], scalar=rstd2[:], in1=shift_b[:], op0=ALU.mult, op1=ALU.add
+            )
+            nc.scalar.activation(out=res[:], in_=res[:], func=ACT.Relu)
+            nc.sync.dma_start(out=out_rows[P * n : P * n + P, :], in_=res[:])
+
+        for n in range(GROUP):
+            normalise(n)
+        for pair in range(W_TILES // 2):
+            quantise_w(pair)
+        bias_b = spread(0)
+        gain_b = spread(1)
+        shift_b = spread(2)
+        for step in range(TILES + GROUP):
+            if step + GROUP < TILES:
+                normalise(step + GROUP)
+            if step < TILES:
+                quantise_y(step // PASSES, step % PASSES)
+            if step >= GROUP:
+                project(step - GROUP)

@@ -21,13 +21,16 @@ PACK = 4
 K_PASS = P * PACK
 PASSES = C // K_PASS
 BLOCKS = C // P
-TILES = TOKENS // P
 W_TILES = H // P
-GROUP = 4
+H_BLOCKS = H // P
+GROUP = 2
 GROUP_TOKENS = GROUP * P
+GROUPS = TOKENS // GROUP_TOKENS
 N_COLS = 512
 HALVES = H // N_COLS
 BN_CHUNK = 512
+
+SCALAR_NORM = 6
 
 FLOPS = 2 * TOKENS * C * H
 
@@ -39,27 +42,30 @@ def tile_graphresblock_pa_kernel(tc, x, pre_w, pre_b, lin1_W, lin1_b, n1_w, n1_b
 
     with ExitStack() as stack:
         const = stack.enter_context(tc.tile_pool(name="const", bufs=1))
-        small = stack.enter_context(tc.tile_pool(name="small", bufs=8))
-        rows_pool = stack.enter_context(tc.tile_pool(name="rows_pool", bufs=12))
-        xn_pool = stack.enter_context(tc.tile_pool(name="xn_pool", bufs=8))
+        small = stack.enter_context(tc.tile_pool(name="small", bufs=4))
+        rows_pool = stack.enter_context(tc.tile_pool(name="rows_pool", bufs=14))
+        xn_pool = stack.enter_context(tc.tile_pool(name="xn_pool", bufs=6))
         stage = stack.enter_context(tc.tile_pool(name="stage", bufs=3))
         y_pool = stack.enter_context(tc.tile_pool(name="y_pool", bufs=2))
-        z_pool = stack.enter_context(tc.tile_pool(name="z_pool", bufs=3))
-        psum_t = stack.enter_context(tc.psum_pool(name="psum_t", bufs=4))
-        psum_acc = stack.enter_context(tc.psum_pool(name="psum_acc", bufs=4))
+        z_pool = stack.enter_context(tc.tile_pool(name="z_pool", bufs=4))
+        out_pool = stack.enter_context(tc.tile_pool(name="out_pool", bufs=4))
+        psum_t = stack.enter_context(tc.psum_pool(name="psum_t", bufs=5))
+        psum_acc = stack.enter_context(tc.psum_pool(name="psum_acc", bufs=3))
 
         ident = const.tile([P, P], F32)
         make_identity(nc, ident[:])
+        wb_rows = const.tile([P, K_PASS], BF16)
+        nc.vector.memset(wb_rows[:].bitcast(I32), 0)
         eps_col = const.tile([P, 1], F32)
         nc.vector.memset(eps_col[:], EPS)
         table_warm = const.tile([P, 1], F32)
         nc.scalar.activation(out=table_warm[:], in_=eps_col[:], func=ACT.Sqrt)
         ones = const.tile([P, P], BF16)
         nc.vector.memset(ones[:], 1.0)
-        wb_rows = const.tile([P, K_PASS], BF16)
-        nc.vector.memset(wb_rows[:].bitcast(I32), 0)
-        vec_rows = const.tile([P, 3, H], BF16)
-        nc.vector.memset(vec_rows[:].rearrange("p v h -> p (v h)").bitcast(I32), 0)
+        nw_rows = const.tile([P, P], BF16)
+        nc.vector.memset(nw_rows[:].bitcast(I32), 0)
+        bias_rows = const.tile([P, H], BF16)
+        nc.vector.memset(bias_rows[:].bitcast(I32), 0)
 
         x_nat = {}
         w_nat = {}
@@ -72,180 +78,325 @@ def tile_graphresblock_pa_kernel(tc, x, pre_w, pre_b, lin1_W, lin1_b, n1_w, n1_b
             w_nat[r] = rows_pool.tile([P, C], BF16, name="w_nat", tag="rows")
             nc.sync.dma_start(out=w_nat[r][:], in_=lin1_W[P * r : P * r + P, :])
 
-        for n in range(GROUP):
-            load_x(n)
         nc.sync.dma_start(out=wb_rows[0:PASSES, :], in_=pre_w.rearrange("(a c) -> a c", c=K_PASS))
         nc.sync.dma_start(out=wb_rows[PASSES : 2 * PASSES, :], in_=pre_b.rearrange("(a c) -> a c", c=K_PASS))
-        for r in range(W_TILES):
+        load_x(0)
+        load_w(0)
+        load_w(1)
+        load_x(1)
+        load_w(2)
+        load_w(3)
+        load_x(2)
+        load_x(3)
+        for r in range(4, W_TILES):
             load_w(r)
-        for v, vec in enumerate((lin1_b, n1_w, n1_b)):
-            nc.sync.dma_start(out=vec_rows[0:1, v, :], in_=vec.rearrange("(o h) -> o h", o=1))
-        for n in range(GROUP, TILES):
+        nc.sync.dma_start(out=bias_rows[0:1, :], in_=lin1_b.rearrange("(o h) -> o h", o=1))
+        nc.sync.dma_start(out=nw_rows[0:H_BLOCKS, :], in_=n1_w.rearrange("(a c) -> a c", c=P))
+        nc.sync.dma_start(out=nw_rows[H_BLOCKS : 2 * H_BLOCKS, :], in_=n1_b.rearrange("(a c) -> a c", c=P))
+        for n in range(4, GROUP * GROUPS):
             load_x(n)
 
-        wb_t = psum_t.tile([P, 2, P], F32, tag="t")
-        for u in range(2):
-            nc.tensor.transpose(wb_t[:, u, :], wb_rows[:].bitcast(F32)[:, u : 2 * P : 2], ident[:])
-        wb_pairs = const.tile([P, 2 * BLOCKS], BF16)
-        nc.vector.tensor_copy(
-            out=wb_pairs[:].bitcast(F32).rearrange("p (a u) -> p a u", u=2),
-            in_=wb_t[:, :, 0 : 2 * PASSES].rearrange("p u a -> p a u"),
-        )
         wb_cols = const.tile([P, 2 * BLOCKS], F32)
-        nc.vector.tensor_copy(out=wb_cols[:], in_=wb_pairs[:])
 
-        xn = {}
+        def spread_pre():
+            wb_t = psum_t.tile([P, 2, P], F32, tag="t")
+            for u in range(2):
+                nc.tensor.transpose(wb_t[:, u, :], wb_rows[:].bitcast(F32)[:, u : 2 * P : 2], ident[:])
+            wb_pairs = const.tile([P, 2 * BLOCKS], BF16)
+            nc.vector.tensor_copy(
+                out=wb_pairs[:].bitcast(F32).rearrange("p (a u) -> p a u", u=2),
+                in_=wb_t[:, :, 0 : 2 * PASSES].rearrange("p u a -> p a u"),
+            )
+            nc.vector.tensor_copy(out=wb_cols[:], in_=wb_pairs[:])
 
-        def normalise(n):
-            stats = small.tile([P, C // BN_CHUNK, 6], F32, name="stats")
-            for s in range(C // BN_CHUNK):
-                nc.vector.bn_stats(out=stats[:, s, :], in_=x_nat[n][:, BN_CHUNK * s : BN_CHUNK * (s + 1)])
-            mean_var = small.tile([P, 2], F32, name="mean_var")
-            nc.vector.bn_aggr(out=mean_var[:], in_=stats[:].rearrange("p s d -> p (s d)"))
-            std = small.tile([P, 1], F32, name="std")
-            nc.scalar.activation(out=std[:], in_=mean_var[:, 1:2], func=ACT.Sqrt, bias=eps_col[:], scale=1.0)
-            rstd = small.tile([P, 1], F32, name="rstd")
-            nc.vector.reciprocal(out=rstd[:], in_=std[:])
-            shift = small.tile([P, 1], F32, name="shift")
-            nc.vector.scalar_tensor_tensor(
-                out=shift[:], in0=mean_var[:, 0:1], scalar=-1.0, in1=rstd[:], op0=ALU.mult, op1=ALU.mult
-            )
-            xn[n] = xn_pool.tile([P, BLOCKS, P], F32, name="xn")
-            nc.scalar.activation(
-                out=xn[n][:].rearrange("p (g t) q -> p g t q", t=PACK),
-                in_=x_nat[n][:].rearrange("p (g q t) -> p g t q", q=P, t=PACK),
-                func=ACT.Identity,
-                scale=rstd[:],
-                bias=shift[:],
-            )
+        nw_cols = const.tile([P, 2 * H_BLOCKS], F32)
+        bias_b = const.tile([P, H], BF16)
+
+        def spread_post():
+            ident_bf = const.tile([P, P], BF16)
+            nc.vector.tensor_copy(out=ident_bf[:], in_=ident[:])
+            nw_t = psum_t.tile([P, P], BF16, tag="t")
+            nc.tensor.transpose(nw_t[:], nw_rows[:], ident_bf[:])
+            nc.vector.tensor_copy(out=nw_cols[:], in_=nw_t[:, 0 : 2 * H_BLOCKS])
+            bias_ps = psum_t.tile([P, H], BF16, tag="t")
+            for hh in range(HALVES):
+                cols = slice(N_COLS * hh, N_COLS * (hh + 1))
+                nc.tensor.matmul(out=bias_ps[:, cols], lhsT=ones[:], rhs=bias_rows[:, cols], start=True, stop=True)
+            nc.scalar.copy(out=bias_b[:], in_=bias_ps[:])
 
         w_words = const.tile([P, PASSES, H], U32, align_bytes=64)
         w_scales = const.tile([P, PASSES, H], U8, align_bytes=64)
+        w_grouped = {}
 
-        def quantise_w(pair):
-            for g in range(PASSES):
-                wt = psum_t.tile([P, 2, 2 * P], F32, tag="t")
+        def turn_w(pair, g):
+            wt = psum_t.tile([P, 2, 2 * P], F32, tag="t")
+            for r in range(2):
+                words = w_nat[2 * pair + r][:].bitcast(F32)
                 for u in range(2):
-                    for r in range(2):
-                        words = w_nat[2 * pair + r][:].bitcast(F32)
-                        first = 2 * P * g + u
-                        nc.tensor.transpose(
-                            wt[:, u, P * r : P * r + P], words[:, first : 2 * P * (g + 1) : 2], ident[:]
-                        )
-                w_grouped = stage.tile([P, 2 * P * PACK], BF16, align_bytes=64, name="w_grouped")
-                nc.scalar.copy(
-                    out=w_grouped[:].bitcast(F32).rearrange("p (h u) -> p h u", u=2),
-                    in_=wt[:].rearrange("p u h -> p h u"),
-                )
-                cols = slice(2 * P * pair, 2 * P * (pair + 1))
-                nc.vector.quantize_mx(
-                    out=w_words[:, g, cols].bitcast(FP8X4), scales=w_scales[:, g, cols], in_=w_grouped[:]
+                    first = 2 * P * g + u
+                    nc.tensor.transpose(wt[:, u, P * r : P * r + P], words[:, first : 2 * P * (g + 1) : 2], ident[:])
+            w_grouped[pair, g] = stage.tile([P, 2 * P * PACK], BF16, align_bytes=64, name="w_grouped")
+            nc.scalar.copy(
+                out=w_grouped[pair, g][:].bitcast(F32).rearrange("p (h u) -> p h u", u=2),
+                in_=wt[:].rearrange("p u h -> p h u"),
+            )
+
+        def quantise_w(pair, g):
+            cols = slice(2 * P * pair, 2 * P * (pair + 1))
+            nc.vector.quantize_mx(
+                out=w_words[:, g, cols].bitcast(FP8X4), scales=w_scales[:, g, cols], in_=w_grouped[pair, g][:]
+            )
+
+        stats = {}
+        mean_var = {}
+        rstd = {}
+        xn = {}
+        shift = {}
+
+        def measure(j, k):
+            i = k // 2
+            if k == 0:
+                mean_var[j] = small.tile([P, GROUP, 2], F32, name="mean_var")
+                rstd[j] = small.tile([P, GROUP], F32, name="rstd")
+            if k % 2 == 0:
+                stats[j] = small.tile([P, C // BN_CHUNK, 6], F32, name="stats")
+            for s in (2 * (k % 2), 2 * (k % 2) + 1):
+                nc.vector.bn_stats(
+                    out=stats[j][:, s, :], in_=x_nat[GROUP * j + i][:, BN_CHUNK * s : BN_CHUNK * (s + 1)]
                 )
 
-        def spread(v):
-            spread_ps = psum_t.tile([P, H], BF16, tag="t")
-            for hh in range(HALVES):
-                cols = slice(N_COLS * hh, N_COLS * (hh + 1))
-                nc.tensor.matmul(out=spread_ps[:, cols], lhsT=ones[:], rhs=vec_rows[:, v, cols], start=True, stop=True)
-            spread_sb = const.tile([P, H], BF16, name="spread_sb%d" % v)
-            nc.scalar.copy(out=spread_sb[:], in_=spread_ps[:])
-            return spread_sb
+        def aggregate(j, k):
+            i = k // 2
+            if k % 2 == 1:
+                nc.vector.bn_aggr(out=mean_var[j][:, i, :], in_=stats[j][:].rearrange("p s d -> p (s d)"))
 
+        def deviation(j, k):
+            if k == 3:
+                std = small.tile([P, GROUP], F32, name="std")
+                nc.scalar.activation(out=std[:], in_=mean_var[j][:, :, 1], func=ACT.Sqrt, bias=eps_col[:], scale=1.0)
+                nc.vector.reciprocal(out=rstd[j][:], in_=std[:])
+                shift[j] = small.tile([P, GROUP], F32, name="shift")
+                nc.vector.scalar_tensor_tensor(
+                    out=shift[j][:], in0=mean_var[j][:, :, 0], scalar=-1.0, in1=rstd[j][:], op0=ALU.mult, op1=ALU.mult
+                )
+
+        def normalise(j, g):
+            xn[j, g] = xn_pool.tile([P, GROUP, PACK, P], F32, name="xn")
+            for i in range(GROUP):
+                chunk = x_nat[GROUP * j + i][:, K_PASS * g : K_PASS * (g + 1)].rearrange("p (q t) -> p t q", t=PACK)
+                if GROUP * j + i < SCALAR_NORM:
+                    nc.scalar.activation(
+                        out=xn[j, g][:, i, :, :],
+                        in_=chunk,
+                        func=ACT.Identity,
+                        scale=rstd[j][:, i : i + 1],
+                        bias=shift[j][:, i : i + 1],
+                    )
+                else:
+                    nc.vector.tensor_scalar(
+                        out=xn[j, g][:, i, :, :],
+                        in0=chunk,
+                        scalar1=rstd[j][:, i : i + 1],
+                        scalar2=shift[j][:, i : i + 1],
+                        op0=ALU.mult,
+                        op1=ALU.add,
+                    )
+
+        x_turned = {}
+        y_planes = {}
+        y_grouped = {}
         y_words = {}
         y_scales = {}
 
-        def quantise_y(group, g):
-            if g == 0:
-                y_words[group] = y_pool.tile([P, PASSES, GROUP_TOKENS], U32, align_bytes=64, name="y_words")
-                y_scales[group] = y_pool.tile([P, PASSES, GROUP_TOKENS], U8, align_bytes=64, name="y_scales")
-            y_planes = stage.tile([P, PACK, GROUP_TOKENS], BF16, name="y_planes")
+        def turn_x(j, g):
+            for b in range(2):
+                x_turned[b] = psum_t.tile([P, 2, GROUP_TOKENS], F32, name="xt", tag="t")
+                for s in range(2):
+                    for i in range(GROUP):
+                        nc.tensor.transpose(
+                            x_turned[b][:, s, P * i : P * i + P], xn[j, g][:, i, 2 * b + s, :], ident[:]
+                        )
+
+        def gain_x(j, g):
+            y_planes[j, g] = stage.tile([P, PACK, GROUP_TOKENS], BF16, name="y_planes")
             for t in range(PACK):
-                j = PACK * g + t
-                xt = psum_t.tile([P, GROUP_TOKENS], F32, tag="t")
-                for i in range(GROUP):
-                    nc.tensor.transpose(xt[:, P * i : P * i + P], xn[GROUP * group + i][:, j, :], ident[:])
+                c = PACK * g + t
                 nc.scalar.activation(
-                    out=y_planes[:, t, :],
-                    in_=xt[:],
+                    out=y_planes[j, g][:, t, :],
+                    in_=x_turned[t // 2][:, t % 2, :],
                     func=ACT.Relu,
-                    scale=wb_cols[:, j : j + 1],
-                    bias=wb_cols[:, BLOCKS + j : BLOCKS + j + 1],
+                    scale=wb_cols[:, c : c + 1],
+                    bias=wb_cols[:, BLOCKS + c : BLOCKS + c + 1],
                 )
-            y_grouped = stage.tile([P, GROUP_TOKENS * PACK], BF16, align_bytes=64, name="y_grouped")
+
+        def interleave_y(j, g):
+            y_grouped[j, g] = stage.tile([P, GROUP_TOKENS * PACK], BF16, align_bytes=64, name="y_grouped")
             nc.vector.tensor_copy(
-                out=y_grouped[:].rearrange("p (c i t) -> p c t i", i=4, t=PACK),
-                in_=y_planes[:].rearrange("p t (c i) -> p c t i", i=4),
-            )
-            nc.vector.quantize_mx(
-                out=y_words[group][:, g, :].bitcast(FP8X4), scales=y_scales[group][:, g, :], in_=y_grouped[:]
+                out=y_grouped[j, g][:].rearrange("p (c i t) -> p c t i", i=4, t=PACK),
+                in_=y_planes[j, g][:].rearrange("p t (c i) -> p c t i", i=4),
             )
 
-        def project(n):
-            group = n // GROUP
-            tok = slice(P * (n % GROUP), P * (n % GROUP) + P)
-            z = z_pool.tile([P, H], F32, name="z")
-            z_sum = small.tile([P, HALVES], F32, name="z_sum")
-            for hh in range(HALVES):
-                cols = slice(N_COLS * hh, N_COLS * (hh + 1))
-                acc = psum_acc.tile([P, N_COLS], F32, name="acc")
-                for g in range(PASSES):
-                    nc.tensor.matmul_mx(
-                        out=acc[:],
-                        lhsT=y_words[group][:, g, tok].bitcast(FP8X4),
-                        lhsT_scale=y_scales[group][:, g, tok],
-                        rhs=w_words[:, g, cols].bitcast(FP8X4),
-                        rhs_scale=w_scales[:, g, cols],
-                        start=(g == 0),
-                        stop=(g == PASSES - 1),
-                    )
-                nc.vector.scalar_tensor_tensor(
-                    out=z[:, cols],
-                    in0=acc[:],
-                    scalar=1.0,
-                    in1=bias_b[:, cols],
-                    op0=ALU.mult,
-                    op1=ALU.add,
-                    accum_out=z_sum[:, hh : hh + 1],
+        def quantise_y(j, g):
+            if g == 0:
+                y_words[j] = y_pool.tile([P, PASSES, GROUP_TOKENS], U32, align_bytes=64, name="y_words")
+                y_scales[j] = y_pool.tile([P, PASSES, GROUP_TOKENS], U8, align_bytes=64, name="y_scales")
+            nc.vector.quantize_mx(
+                out=y_words[j][:, g, :].bitcast(FP8X4), scales=y_scales[j][:, g, :], in_=y_grouped[j, g][:]
+            )
+
+        acc = {}
+        z = {}
+        z_sum = {}
+        neg_mean = {}
+        rstd2 = {}
+        sum_sq = {}
+
+        def project(j, k):
+            i, hh = k // 2, k % 2
+            tok = slice(P * i, P * i + P)
+            cols = slice(N_COLS * hh, N_COLS * (hh + 1))
+            acc[j, k] = psum_acc.tile([P, N_COLS], F32, name="acc")
+            for g in range(PASSES):
+                nc.tensor.matmul_mx(
+                    out=acc[j, k][:],
+                    lhsT=y_words[j][:, g, tok].bitcast(FP8X4),
+                    lhsT_scale=y_scales[j][:, g, tok],
+                    rhs=w_words[:, g, cols].bitcast(FP8X4),
+                    rhs_scale=w_scales[:, g, cols],
+                    start=(g == 0),
+                    stop=(g == PASSES - 1),
                 )
-            neg_mean = small.tile([P, 1], F32, name="neg_mean")
+
+        def add_bias(j, k):
+            i, hh = k // 2, k % 2
+            cols = slice(N_COLS * hh, N_COLS * (hh + 1))
+            if hh == 0:
+                z[j, i] = z_pool.tile([P, H], F32, name="z")
+                z_sum[j, i] = small.tile([P, HALVES], F32, name="z_sum")
+            nc.vector.scalar_tensor_tensor(
+                out=z[j, i][:, cols],
+                in0=acc[j, k][:],
+                scalar=1.0,
+                in1=bias_b[:, cols],
+                op0=ALU.mult,
+                op1=ALU.add,
+                accum_out=z_sum[j, i][:, hh : hh + 1],
+            )
+
+        def centre(j, i):
+            neg_mean[j, i] = small.tile([P, 1], F32, name="neg_mean")
             nc.vector.tensor_scalar(
-                out=neg_mean[:],
-                in0=z_sum[:, 0:1],
-                scalar1=z_sum[:, 1:2],
+                out=neg_mean[j, i][:],
+                in0=z_sum[j, i][:, 0:1],
+                scalar1=z_sum[j, i][:, 1:2],
                 scalar2=-1.0 / H,
                 op0=ALU.add,
                 op1=ALU.mult,
             )
-            squares = z_pool.tile([P, H], BF16, name="squares")
-            sum_sq = small.tile([P, 1], F32, name="sum_sq")
-            nc.scalar.activation(
-                out=squares[:], in_=z[:], func=ACT.Square, bias=neg_mean[:], scale=1.0, accum_out=sum_sq[:]
-            )
-            std2 = small.tile([P, 1], F32, name="std2")
-            nc.scalar.activation(out=std2[:], in_=sum_sq[:], func=ACT.Sqrt, bias=eps_col[:], scale=1.0 / H)
-            rstd2 = small.tile([P, 1], F32, name="rstd2")
-            nc.vector.reciprocal(out=rstd2[:], in_=std2[:])
-            res = z_pool.tile([P, H], F32, name="res")
-            nc.vector.scalar_tensor_tensor(
-                out=res[:], in0=z[:], scalar=neg_mean[:], in1=gain_b[:], op0=ALU.add, op1=ALU.mult
-            )
-            nc.vector.scalar_tensor_tensor(
-                out=res[:], in0=res[:], scalar=rstd2[:], in1=shift_b[:], op0=ALU.mult, op1=ALU.add
-            )
-            nc.scalar.activation(out=res[:], in_=res[:], func=ACT.Relu)
-            nc.sync.dma_start(out=out_rows[P * n : P * n + P, :], in_=res[:])
 
-        for n in range(GROUP):
-            normalise(n)
-        for pair in range(W_TILES // 2):
-            quantise_w(pair)
-        bias_b = spread(0)
-        gain_b = spread(1)
-        shift_b = spread(2)
-        for step in range(TILES + GROUP):
-            if step + GROUP < TILES:
-                normalise(step + GROUP)
-            if step < TILES:
-                quantise_y(step // PASSES, step % PASSES)
-            if step >= GROUP:
-                project(step - GROUP)
+        def spread_of(j, i):
+            squares = stage.tile([P, H], BF16, name="squares")
+            sum_sq[j, i] = small.tile([P, 1], F32, name="sum_sq")
+            nc.scalar.activation(
+                out=squares[:], in_=z[j, i][:], func=ACT.Square, bias=neg_mean[j, i][:], scale=1.0, accum_out=sum_sq[j, i][:]
+            )
+
+        zn = {}
+
+        def normalise_z(j, i):
+            std2 = small.tile([P, 1], F32, name="std2")
+            nc.scalar.activation(
+                out=std2[:], in_=sum_sq[j, i][:], func=ACT.Sqrt, bias=eps_col[:], scale=1.0 / H
+            )
+            rstd2[j, i] = small.tile([P, 1], F32, name="rstd2")
+            nc.vector.reciprocal(out=rstd2[j, i][:], in_=std2[:])
+            zn[j, i] = z_pool.tile([P, H], F32, name="zn")
+            nc.vector.tensor_scalar(
+                out=zn[j, i][:],
+                in0=z[j, i][:],
+                scalar1=neg_mean[j, i][:],
+                scalar2=rstd2[j, i][:],
+                op0=ALU.add,
+                op1=ALU.mult,
+            )
+
+        z_turned = {}
+        res_t = {}
+        res_back = {}
+
+        def turn_z(j, k):
+            z_turned[j, k] = psum_t.tile([P, 2, GROUP_TOKENS], F32, name="zt", tag="t")
+            for s in range(2):
+                hb = 2 * k + s
+                for i in range(GROUP):
+                    nc.tensor.transpose(
+                        z_turned[j, k][:, s, P * i : P * i + P], zn[j, i][:, P * hb : P * hb + P], ident[:]
+                    )
+
+        def gain_z(j, k):
+            if k == 0:
+                res_t[j] = out_pool.tile([P, H_BLOCKS, GROUP_TOKENS], F32, name="res_t", bufs=2)
+            for s in range(2):
+                hb = 2 * k + s
+                nc.scalar.activation(
+                    out=res_t[j][:, hb, :],
+                    in_=z_turned[j, k][:, s, :],
+                    func=ACT.Relu,
+                    scale=nw_cols[:, hb : hb + 1],
+                    bias=nw_cols[:, H_BLOCKS + hb : H_BLOCKS + hb + 1],
+                )
+
+        def turn_back(j, k):
+            hh, i = k // 2, k % 2
+            res_back[j, k] = psum_t.tile([P, N_COLS], F32, name="res_back", tag="t")
+            for b in range(4):
+                nc.tensor.transpose(
+                    res_back[j, k][:, P * b : P * b + P], res_t[j][:, 4 * hh + b, P * i : P * i + P], ident[:]
+                )
+
+        def store(j, k):
+            hh, i = k // 2, k % 2
+            res = out_pool.tile([P, N_COLS], F32, name="res")
+            if k % 2 == 0:
+                nc.vector.tensor_copy(out=res[:], in_=res_back[j, k][:])
+            else:
+                nc.scalar.copy(out=res[:], in_=res_back[j, k][:])
+            n = GROUP * j + i
+            nc.sync.dma_start(out=out_rows[P * n : P * n + P, N_COLS * hh : N_COLS * (hh + 1)], in_=res[:])
+
+        def at(step, lag, count, work):
+            d = step - lag
+            if d >= 0 and d // count < GROUPS:
+                work(d // count, d % count)
+
+        def every_other(step, lag, work):
+            d = step - lag
+            if d >= 0 and d % 2 == 0 and d // 4 < GROUPS:
+                work(d // 4, d % 4 // 2)
+
+        w_order = [(pair, g) for pair in range(W_TILES // 2) for g in range(PASSES)]
+        spread_pre()
+        for step in range(4 * GROUPS + 21):
+            at(step, 4, 4, normalise)
+            every_other(step, 13, normalise_z)
+            at(step, 5, 4, turn_x)
+            at(step, 16, 4, turn_z)
+            at(step, 18, 4, turn_back)
+            for pair, g in w_order[2 * step : 2 * step + 2]:
+                turn_w(pair, g)
+            at(step, 10, 4, project)
+            at(step, 0, 4, measure)
+            at(step, 11, 4, add_bias)
+            at(step, 5, 4, gain_x)
+            at(step, 16, 4, gain_z)
+            at(step, 0, 4, aggregate)
+            at(step, 0, 4, deviation)
+            at(step, 6, 4, interleave_y)
+            for pair, g in w_order[2 * step : 2 * step + 2]:
+                quantise_w(pair, g)
+            every_other(step, 12, centre)
+            at(step, 18, 4, store)
+            at(step, 6, 4, quantise_y)
+            every_other(step, 12, spread_of)
+            if step == 8:
+                spread_post()

@@ -30,7 +30,9 @@ N_COLS = 512
 HALVES = H // N_COLS
 BN_CHUNK = 512
 
-SCALAR_NORM = 6
+SCALAR_NORM = 8
+
+STRAIGHT = 5
 
 FLOPS = 2 * TOKENS * C * H
 
@@ -64,8 +66,8 @@ def tile_graphresblock_pa_kernel(tc, x, pre_w, pre_b, lin1_W, lin1_b, n1_w, n1_b
         nc.vector.memset(ones[:], 1.0)
         nw_rows = const.tile([P, P], BF16)
         nc.vector.memset(nw_rows[:].bitcast(I32), 0)
-        bias_rows = const.tile([P, H], BF16)
-        nc.vector.memset(bias_rows[:].bitcast(I32), 0)
+        vec_rows = const.tile([P, 3, H], BF16)
+        nc.vector.memset(vec_rows[:].rearrange("p v h -> p (v h)").bitcast(I32), 0)
 
         x_nat = {}
         w_nat = {}
@@ -90,7 +92,8 @@ def tile_graphresblock_pa_kernel(tc, x, pre_w, pre_b, lin1_W, lin1_b, n1_w, n1_b
         load_x(3)
         for r in range(4, W_TILES):
             load_w(r)
-        nc.sync.dma_start(out=bias_rows[0:1, :], in_=lin1_b.rearrange("(o h) -> o h", o=1))
+        for v, vec in enumerate((lin1_b, n1_w, n1_b)):
+            nc.sync.dma_start(out=vec_rows[0:1, v, :], in_=vec.rearrange("(o h) -> o h", o=1))
         nc.sync.dma_start(out=nw_rows[0:H_BLOCKS, :], in_=n1_w.rearrange("(a c) -> a c", c=P))
         nc.sync.dma_start(out=nw_rows[H_BLOCKS : 2 * H_BLOCKS, :], in_=n1_b.rearrange("(a c) -> a c", c=P))
         for n in range(4, GROUP * GROUPS):
@@ -110,7 +113,12 @@ def tile_graphresblock_pa_kernel(tc, x, pre_w, pre_b, lin1_W, lin1_b, n1_w, n1_b
             nc.vector.tensor_copy(out=wb_cols[:], in_=wb_pairs[:])
 
         nw_cols = const.tile([P, 2 * H_BLOCKS], F32)
-        bias_b = const.tile([P, H], BF16)
+        spread_rows = {}
+        for name in ("bias", "gain", "shift"):
+            spread_rows[name] = const.tile([P, H], BF16, name="spread_" + name)
+        bias_b = spread_rows["bias"]
+        gain_b = spread_rows["gain"]
+        shift_b = spread_rows["shift"]
 
         def spread_post():
             ident_bf = const.tile([P, P], BF16)
@@ -118,18 +126,26 @@ def tile_graphresblock_pa_kernel(tc, x, pre_w, pre_b, lin1_W, lin1_b, n1_w, n1_b
             nw_t = psum_t.tile([P, P], BF16, tag="t")
             nc.tensor.transpose(nw_t[:], nw_rows[:], ident_bf[:])
             nc.vector.tensor_copy(out=nw_cols[:], in_=nw_t[:, 0 : 2 * H_BLOCKS])
+            spread_vec(0, bias_b)
+
+        def spread_vec(v, dst):
             bias_ps = psum_t.tile([P, H], BF16, tag="t")
             for hh in range(HALVES):
                 cols = slice(N_COLS * hh, N_COLS * (hh + 1))
-                nc.tensor.matmul(out=bias_ps[:, cols], lhsT=ones[:], rhs=bias_rows[:, cols], start=True, stop=True)
-            nc.scalar.copy(out=bias_b[:], in_=bias_ps[:])
+                nc.tensor.matmul(out=bias_ps[:, cols], lhsT=ones[:], rhs=vec_rows[:, v, cols], start=True, stop=True)
+            nc.scalar.copy(out=dst[:], in_=bias_ps[:])
 
         w_words = const.tile([P, PASSES, H], U32, align_bytes=64)
         w_scales = const.tile([P, PASSES, H], U8, align_bytes=64)
         w_grouped = {}
 
+        def warm(dst):
+            nc.tensor.matmul(out=dst, lhsT=ident[:], rhs=ident[:], start=True, stop=True)
+
         def turn_w(pair, g):
             wt = psum_t.tile([P, 2, 2 * P], F32, tag="t")
+            for r in range(2):
+                warm(wt[:, 0, 0:P])
             for r in range(2):
                 words = w_nat[2 * pair + r][:].bitcast(F32)
                 for u in range(2):
@@ -294,6 +310,13 @@ def tile_graphresblock_pa_kernel(tc, x, pre_w, pre_b, lin1_W, lin1_b, n1_w, n1_b
                 op1=ALU.mult,
             )
 
+        def gain_early(j, i):
+            if j >= STRAIGHT:
+                zn[j, i] = z_pool.tile([P, H], F32, name="zn")
+                nc.vector.scalar_tensor_tensor(
+                    out=zn[j, i][:], in0=z[j, i][:], scalar=neg_mean[j, i][:], in1=gain_b[:], op0=ALU.add, op1=ALU.mult
+                )
+
         def spread_of(j, i):
             squares = stage.tile([P, H], BF16, name="squares")
             sum_sq[j, i] = small.tile([P, 1], F32, name="sum_sq")
@@ -310,6 +333,14 @@ def tile_graphresblock_pa_kernel(tc, x, pre_w, pre_b, lin1_W, lin1_b, n1_w, n1_b
             )
             rstd2[j, i] = small.tile([P, 1], F32, name="rstd2")
             nc.vector.reciprocal(out=rstd2[j, i][:], in_=std2[:])
+            if j >= STRAIGHT:
+                nc.vector.scalar_tensor_tensor(
+                    out=zn[j, i][:], in0=zn[j, i][:], scalar=rstd2[j, i][:], in1=shift_b[:], op0=ALU.mult, op1=ALU.add
+                )
+                nc.vector.tensor_scalar_max(out=zn[j, i][:], in0=zn[j, i][:], scalar1=0.0)
+                n = GROUP * j + i
+                nc.sync.dma_start(out=out_rows[P * n : P * n + P, :], in_=zn[j, i][:])
+                return
             zn[j, i] = z_pool.tile([P, H], F32, name="zn")
             nc.vector.tensor_scalar(
                 out=zn[j, i][:],
@@ -325,6 +356,8 @@ def tile_graphresblock_pa_kernel(tc, x, pre_w, pre_b, lin1_W, lin1_b, n1_w, n1_b
         res_back = {}
 
         def turn_z(j, k):
+            if j >= STRAIGHT:
+                return
             z_turned[j, k] = psum_t.tile([P, 2, GROUP_TOKENS], F32, name="zt", tag="t")
             for s in range(2):
                 hb = 2 * k + s
@@ -334,6 +367,8 @@ def tile_graphresblock_pa_kernel(tc, x, pre_w, pre_b, lin1_W, lin1_b, n1_w, n1_b
                     )
 
         def gain_z(j, k):
+            if j >= STRAIGHT:
+                return
             if k == 0:
                 res_t[j] = out_pool.tile([P, H_BLOCKS, GROUP_TOKENS], F32, name="res_t", bufs=2)
             for s in range(2):
@@ -347,6 +382,8 @@ def tile_graphresblock_pa_kernel(tc, x, pre_w, pre_b, lin1_W, lin1_b, n1_w, n1_b
                 )
 
         def turn_back(j, k):
+            if j >= STRAIGHT:
+                return
             hh, i = k // 2, k % 2
             res_back[j, k] = psum_t.tile([P, N_COLS], F32, name="res_back", tag="t")
             for b in range(4):
@@ -355,9 +392,11 @@ def tile_graphresblock_pa_kernel(tc, x, pre_w, pre_b, lin1_W, lin1_b, n1_w, n1_b
                 )
 
         def store(j, k):
+            if j >= STRAIGHT:
+                return
             hh, i = k // 2, k % 2
             res = out_pool.tile([P, N_COLS], F32, name="res")
-            if k % 2 == 0:
+            if k == 0:
                 nc.vector.tensor_copy(out=res[:], in_=res_back[j, k][:])
             else:
                 nc.scalar.copy(out=res[:], in_=res_back[j, k][:])
@@ -398,5 +437,9 @@ def tile_graphresblock_pa_kernel(tc, x, pre_w, pre_b, lin1_W, lin1_b, n1_w, n1_b
             at(step, 18, 4, store)
             at(step, 6, 4, quantise_y)
             every_other(step, 12, spread_of)
+            every_other(step, 12, gain_early)
+            if step == 18:
+                spread_vec(1, gain_b)
+                spread_vec(2, shift_b)
             if step == 8:
                 spread_post()

@@ -30,7 +30,7 @@ N_COLS = 512
 HALVES = H // N_COLS
 BN_CHUNK = 512
 
-SCALAR_NORM = 8
+SCALAR_NORM = 6
 
 STRAIGHT = 5
 
@@ -56,14 +56,14 @@ def tile_graphresblock_pa_kernel(tc, x, pre_w, pre_b, lin1_W, lin1_b, n1_w, n1_b
 
         ident = const.tile([P, P], F32)
         make_identity(nc, ident[:])
+        ones = const.tile([P, N_COLS], BF16)
+        nc.vector.memset(ones[:], 1.0)
         wb_rows = const.tile([P, K_PASS], BF16)
         nc.vector.memset(wb_rows[:].bitcast(I32), 0)
         eps_col = const.tile([P, 1], F32)
         nc.vector.memset(eps_col[:], EPS)
         table_warm = const.tile([P, 1], F32)
         nc.scalar.activation(out=table_warm[:], in_=eps_col[:], func=ACT.Sqrt)
-        ones = const.tile([P, P], BF16)
-        nc.vector.memset(ones[:], 1.0)
         nw_rows = const.tile([P, P], BF16)
         nc.vector.memset(nw_rows[:].bitcast(I32), 0)
         vec_rows = const.tile([P, 3, H], BF16)
@@ -132,7 +132,7 @@ def tile_graphresblock_pa_kernel(tc, x, pre_w, pre_b, lin1_W, lin1_b, n1_w, n1_b
             bias_ps = psum_t.tile([P, H], BF16, tag="t")
             for hh in range(HALVES):
                 cols = slice(N_COLS * hh, N_COLS * (hh + 1))
-                nc.tensor.matmul(out=bias_ps[:, cols], lhsT=ones[:], rhs=vec_rows[:, v, cols], start=True, stop=True)
+                nc.tensor.matmul(out=bias_ps[:, cols], lhsT=ones[:, 0:P], rhs=vec_rows[:, v, cols], start=True, stop=True)
             nc.scalar.copy(out=dst[:], in_=bias_ps[:])
 
         w_words = const.tile([P, PASSES, H], U32, align_bytes=64)
@@ -140,12 +140,12 @@ def tile_graphresblock_pa_kernel(tc, x, pre_w, pre_b, lin1_W, lin1_b, n1_w, n1_b
         w_grouped = {}
 
         def warm(dst):
-            nc.tensor.matmul(out=dst, lhsT=ident[:], rhs=ident[:], start=True, stop=True)
+            nc.tensor.matmul(out=dst, lhsT=ones[:, 0:P], rhs=ones[:], start=True, stop=True)
 
         def turn_w(pair, g):
             wt = psum_t.tile([P, 2, 2 * P], F32, tag="t")
             for r in range(2):
-                warm(wt[:, 0, 0:P])
+                warm(wt[:].rearrange("p u h -> p (u h)"))
             for r in range(2):
                 words = w_nat[2 * pair + r][:].bitcast(F32)
                 for u in range(2):

@@ -74,7 +74,10 @@ def tile_graphresblock_pa_kernel(tc, x, pre_w, pre_b, lin1_W, lin1_b, n1_w, n1_b
 
         def load_x(n):
             x_nat[n] = rows_pool.tile([P, C], BF16, name="x_nat", tag="rows")
-            nc.sync.dma_start(out=x_nat[n][:], in_=x_rows[P * n : P * n + P, :])
+            pieces = 2 if n == 0 else 1
+            for s in range(pieces):
+                cols = slice(C // pieces * s, C // pieces * (s + 1))
+                nc.sync.dma_start(out=x_nat[n][:, cols], in_=x_rows[P * n : P * n + P, cols])
 
         def load_w(r):
             w_nat[r] = rows_pool.tile([P, C], BF16, name="w_nat", tag="rows")
@@ -139,13 +142,13 @@ def tile_graphresblock_pa_kernel(tc, x, pre_w, pre_b, lin1_W, lin1_b, n1_w, n1_b
         w_scales = const.tile([P, PASSES, H], U8, align_bytes=64)
         w_grouped = {}
 
-        def warm(dst):
-            nc.tensor.matmul(out=dst, lhsT=ones[:, 0:P], rhs=ones[:], start=True, stop=True)
+        warm_ps = psum_acc.tile([P, N_COLS], F32, name="warm_ps", tag="acc")
+
+        def warm(src):
+            nc.tensor.matmul(out=warm_ps[:], lhsT=ones[:, 0:P], rhs=src, start=True, stop=True)
 
         def turn_w(pair, g):
             wt = psum_t.tile([P, 2, 2 * P], F32, tag="t")
-            for r in range(2):
-                warm(wt[:].rearrange("p u h -> p (u h)"))
             for r in range(2):
                 words = w_nat[2 * pair + r][:].bitcast(F32)
                 for u in range(2):
@@ -156,6 +159,9 @@ def tile_graphresblock_pa_kernel(tc, x, pre_w, pre_b, lin1_W, lin1_b, n1_w, n1_b
                 out=w_grouped[pair, g][:].bitcast(F32).rearrange("p (h u) -> p h u", u=2),
                 in_=wt[:].rearrange("p u h -> p h u"),
             )
+
+        def warm_w(pair, g):
+            warm(w_grouped[pair, g][:, 0:N_COLS])
 
         def quantise_w(pair, g):
             cols = slice(2 * P * pair, 2 * P * (pair + 1))
@@ -271,7 +277,7 @@ def tile_graphresblock_pa_kernel(tc, x, pre_w, pre_b, lin1_W, lin1_b, n1_w, n1_b
             i, hh = k // 2, k % 2
             tok = slice(P * i, P * i + P)
             cols = slice(N_COLS * hh, N_COLS * (hh + 1))
-            acc[j, k] = psum_acc.tile([P, N_COLS], F32, name="acc")
+            acc[j, k] = psum_acc.tile([P, N_COLS], F32, name="acc", tag="acc")
             for g in range(PASSES):
                 nc.tensor.matmul_mx(
                     out=acc[j, k][:],
@@ -337,9 +343,11 @@ def tile_graphresblock_pa_kernel(tc, x, pre_w, pre_b, lin1_W, lin1_b, n1_w, n1_b
                 nc.vector.scalar_tensor_tensor(
                     out=zn[j, i][:], in0=zn[j, i][:], scalar=rstd2[j, i][:], in1=shift_b[:], op0=ALU.mult, op1=ALU.add
                 )
-                nc.vector.tensor_scalar_max(out=zn[j, i][:], in0=zn[j, i][:], scalar1=0.0)
                 n = GROUP * j + i
-                nc.sync.dma_start(out=out_rows[P * n : P * n + P, :], in_=zn[j, i][:])
+                for hh in range(HALVES):
+                    cols = slice(N_COLS * hh, N_COLS * (hh + 1))
+                    nc.vector.tensor_scalar_max(out=zn[j, i][:, cols], in0=zn[j, i][:, cols], scalar1=0.0)
+                    nc.sync.dma_start(out=out_rows[P * n : P * n + P, cols], in_=zn[j, i][:, cols])
                 return
             zn[j, i] = z_pool.tile([P, H], F32, name="zn")
             nc.vector.tensor_scalar(
@@ -414,6 +422,8 @@ def tile_graphresblock_pa_kernel(tc, x, pre_w, pre_b, lin1_W, lin1_b, n1_w, n1_b
                 work(d // 4, d % 4 // 2)
 
         w_order = [(pair, g) for pair in range(W_TILES // 2) for g in range(PASSES)]
+        for r in range(4):
+            warm(ones[:])
         spread_pre()
         for step in range(4 * GROUPS + 21):
             at(step, 4, 4, normalise)
@@ -433,6 +443,7 @@ def tile_graphresblock_pa_kernel(tc, x, pre_w, pre_b, lin1_W, lin1_b, n1_w, n1_b
             at(step, 6, 4, interleave_y)
             for pair, g in w_order[2 * step : 2 * step + 2]:
                 quantise_w(pair, g)
+                warm_w(pair, g)
             every_other(step, 12, centre)
             at(step, 18, 4, store)
             at(step, 6, 4, quantise_y)

@@ -45,7 +45,7 @@ def tile_graphresblock_pa_kernel(tc, x, pre_w, pre_b, lin1_W, lin1_b, n1_w, n1_b
     with ExitStack() as stack:
         const = stack.enter_context(tc.tile_pool(name="const", bufs=1))
         small = stack.enter_context(tc.tile_pool(name="small", bufs=4))
-        rows_pool = stack.enter_context(tc.tile_pool(name="rows_pool", bufs=14))
+        rows_pool = stack.enter_context(tc.tile_pool(name="rows_pool", bufs=8))
         xn_pool = stack.enter_context(tc.tile_pool(name="xn_pool", bufs=6))
         stage = stack.enter_context(tc.tile_pool(name="stage", bufs=3))
         y_pool = stack.enter_context(tc.tile_pool(name="y_pool", bufs=2))
@@ -86,9 +86,9 @@ def tile_graphresblock_pa_kernel(tc, x, pre_w, pre_b, lin1_W, lin1_b, n1_w, n1_b
         nc.sync.dma_start(out=wb_rows[0:PASSES, :], in_=pre_w.rearrange("(a c) -> a c", c=K_PASS))
         nc.sync.dma_start(out=wb_rows[PASSES : 2 * PASSES, :], in_=pre_b.rearrange("(a c) -> a c", c=K_PASS))
         load_x(0)
+        load_x(1)
         load_w(0)
         load_w(1)
-        load_x(1)
         load_w(2)
         load_w(3)
         load_x(2)
@@ -193,13 +193,22 @@ def tile_graphresblock_pa_kernel(tc, x, pre_w, pre_b, lin1_W, lin1_b, n1_w, n1_b
                 nc.vector.bn_aggr(out=mean_var[j][:, i, :], in_=stats[j][:].rearrange("p s d -> p (s d)"))
 
         def deviation(j, k):
-            if k == 3:
-                std = small.tile([P, GROUP], F32, name="std")
-                nc.scalar.activation(out=std[:], in_=mean_var[j][:, :, 1], func=ACT.Sqrt, bias=eps_col[:], scale=1.0)
-                nc.vector.reciprocal(out=rstd[j][:], in_=std[:])
+            if k == 1:
                 shift[j] = small.tile([P, GROUP], F32, name="shift")
+            if k == 3 or (k == 1 and j == 0):
+                sel = slice(k // 2, k // 2 + 1) if j == 0 else slice(0, GROUP)
+                std = small.tile([P, GROUP], F32, name="std")
+                nc.scalar.activation(
+                    out=std[:, sel], in_=mean_var[j][:, sel, 1], func=ACT.Sqrt, bias=eps_col[:], scale=1.0
+                )
+                nc.vector.reciprocal(out=rstd[j][:, sel], in_=std[:, sel])
                 nc.vector.scalar_tensor_tensor(
-                    out=shift[j][:], in0=mean_var[j][:, :, 0], scalar=-1.0, in1=rstd[j][:], op0=ALU.mult, op1=ALU.mult
+                    out=shift[j][:, sel],
+                    in0=mean_var[j][:, sel, 0],
+                    scalar=-1.0,
+                    in1=rstd[j][:, sel],
+                    op0=ALU.mult,
+                    op1=ALU.mult,
                 )
 
         def normalise(j, g):

@@ -30,6 +30,8 @@ N_COLS = 512
 HALVES = H // N_COLS
 BN_CHUNK = 512
 
+LOADS = "x0 w0 x1 w1 w2 w3 x2 x3 w4 w5 w6 w7"
+PIECES = (4, 2)
 SCALAR_NORM = 6
 
 STRAIGHT = 5
@@ -74,7 +76,7 @@ def tile_graphresblock_pa_kernel(tc, x, pre_w, pre_b, lin1_W, lin1_b, n1_w, n1_b
 
         def load_x(n):
             x_nat[n] = rows_pool.tile([P, C], BF16, name="x_nat", tag="rows")
-            pieces = 2 if n == 0 else 1
+            pieces = PIECES[n] if n < len(PIECES) else 1
             for s in range(pieces):
                 cols = slice(C // pieces * s, C // pieces * (s + 1))
                 nc.sync.dma_start(out=x_nat[n][:, cols], in_=x_rows[P * n : P * n + P, cols])
@@ -85,16 +87,8 @@ def tile_graphresblock_pa_kernel(tc, x, pre_w, pre_b, lin1_W, lin1_b, n1_w, n1_b
 
         nc.sync.dma_start(out=wb_rows[0:PASSES, :], in_=pre_w.rearrange("(a c) -> a c", c=K_PASS))
         nc.sync.dma_start(out=wb_rows[PASSES : 2 * PASSES, :], in_=pre_b.rearrange("(a c) -> a c", c=K_PASS))
-        load_x(0)
-        load_x(1)
-        load_w(0)
-        load_w(1)
-        load_w(2)
-        load_w(3)
-        load_x(2)
-        load_x(3)
-        for r in range(4, W_TILES):
-            load_w(r)
+        for item in LOADS.split():
+            (load_x if item[0] == "x" else load_w)(int(item[1:]))
         for v, vec in enumerate((lin1_b, n1_w, n1_b)):
             nc.sync.dma_start(out=vec_rows[0:1, v, :], in_=vec.rearrange("(o h) -> o h", o=1))
         nc.sync.dma_start(out=nw_rows[0:H_BLOCKS, :], in_=n1_w.rearrange("(a c) -> a c", c=P))
@@ -435,13 +429,13 @@ def tile_graphresblock_pa_kernel(tc, x, pre_w, pre_b, lin1_W, lin1_b, n1_w, n1_b
             warm(ones[:])
         spread_pre()
         for step in range(4 * GROUPS + 21):
+            for pair, g in w_order[4 * step : 4 * step + 4]:
+                turn_w(pair, g)
             at(step, 4, 4, normalise)
             every_other(step, 13, normalise_z)
             at(step, 5, 4, turn_x)
             at(step, 16, 4, turn_z)
             at(step, 18, 4, turn_back)
-            for pair, g in w_order[2 * step : 2 * step + 2]:
-                turn_w(pair, g)
             at(step, 10, 4, project)
             at(step, 0, 4, measure)
             at(step, 11, 4, add_bias)
@@ -450,7 +444,7 @@ def tile_graphresblock_pa_kernel(tc, x, pre_w, pre_b, lin1_W, lin1_b, n1_w, n1_b
             at(step, 0, 4, aggregate)
             at(step, 0, 4, deviation)
             at(step, 6, 4, interleave_y)
-            for pair, g in w_order[2 * step : 2 * step + 2]:
+            for pair, g in w_order[4 * step : 4 * step + 4]:
                 quantise_w(pair, g)
                 warm_w(pair, g)
             every_other(step, 12, centre)

@@ -32,7 +32,8 @@ BN_CHUNK = 512
 
 LOADS = "x0 w0 x1 w1 w2 w3 x2 x3 w4 w5 w6 w7"
 PIECES = (4, 2)
-SCALAR_NORM = 6
+FINE = 1
+SCALAR_NORM = 7
 
 STRAIGHT = 5
 
@@ -48,7 +49,7 @@ def tile_graphresblock_pa_kernel(tc, x, pre_w, pre_b, lin1_W, lin1_b, n1_w, n1_b
         const = stack.enter_context(tc.tile_pool(name="const", bufs=1))
         small = stack.enter_context(tc.tile_pool(name="small", bufs=4))
         rows_pool = stack.enter_context(tc.tile_pool(name="rows_pool", bufs=8))
-        xn_pool = stack.enter_context(tc.tile_pool(name="xn_pool", bufs=6))
+        xn_pool = stack.enter_context(tc.tile_pool(name="xn_pool", bufs=4))
         stage = stack.enter_context(tc.tile_pool(name="stage", bufs=3))
         y_pool = stack.enter_context(tc.tile_pool(name="y_pool", bufs=2))
         z_pool = stack.enter_context(tc.tile_pool(name="z_pool", bufs=4))
@@ -68,8 +69,8 @@ def tile_graphresblock_pa_kernel(tc, x, pre_w, pre_b, lin1_W, lin1_b, n1_w, n1_b
         nc.scalar.activation(out=table_warm[:], in_=eps_col[:], func=ACT.Sqrt)
         nw_rows = const.tile([P, P], BF16)
         nc.vector.memset(nw_rows[:].bitcast(I32), 0)
-        vec_rows = const.tile([P, 3, H], BF16)
-        nc.vector.memset(vec_rows[:].rearrange("p v h -> p (v h)").bitcast(I32), 0)
+        bias_rows = const.tile([P, H], BF16)
+        nc.vector.memset(bias_rows[:].bitcast(I32), 0)
 
         x_nat = {}
         w_nat = {}
@@ -89,12 +90,15 @@ def tile_graphresblock_pa_kernel(tc, x, pre_w, pre_b, lin1_W, lin1_b, n1_w, n1_b
         nc.sync.dma_start(out=wb_rows[PASSES : 2 * PASSES, :], in_=pre_b.rearrange("(a c) -> a c", c=K_PASS))
         for item in LOADS.split():
             (load_x if item[0] == "x" else load_w)(int(item[1:]))
-        for v, vec in enumerate((lin1_b, n1_w, n1_b)):
-            nc.sync.dma_start(out=vec_rows[0:1, v, :], in_=vec.rearrange("(o h) -> o h", o=1))
+        nc.sync.dma_start(out=bias_rows[0:1, :], in_=lin1_b.rearrange("(o h) -> o h", o=1))
         nc.sync.dma_start(out=nw_rows[0:H_BLOCKS, :], in_=n1_w.rearrange("(a c) -> a c", c=P))
         nc.sync.dma_start(out=nw_rows[H_BLOCKS : 2 * H_BLOCKS, :], in_=n1_b.rearrange("(a c) -> a c", c=P))
         for n in range(4, GROUP * GROUPS):
             load_x(n)
+        gain_b = const.tile([P, H], BF16)
+        nc.sync.dma_start(out=gain_b[:], in_=n1_w.partition_broadcast(P))
+        shift_b = const.tile([P, H], BF16)
+        nc.sync.dma_start(out=shift_b[:], in_=n1_b.partition_broadcast(P))
 
         wb_cols = const.tile([P, 2 * BLOCKS], F32)
 
@@ -110,12 +114,7 @@ def tile_graphresblock_pa_kernel(tc, x, pre_w, pre_b, lin1_W, lin1_b, n1_w, n1_b
             nc.vector.tensor_copy(out=wb_cols[:], in_=wb_pairs[:])
 
         nw_cols = const.tile([P, 2 * H_BLOCKS], F32)
-        spread_rows = {}
-        for name in ("bias", "gain", "shift"):
-            spread_rows[name] = const.tile([P, H], BF16, name="spread_" + name)
-        bias_b = spread_rows["bias"]
-        gain_b = spread_rows["gain"]
-        shift_b = spread_rows["shift"]
+        bias_b = const.tile([P, H], BF16)
 
         def spread_post():
             ident_bf = const.tile([P, P], BF16)
@@ -123,14 +122,11 @@ def tile_graphresblock_pa_kernel(tc, x, pre_w, pre_b, lin1_W, lin1_b, n1_w, n1_b
             nw_t = psum_t.tile([P, P], BF16, tag="t")
             nc.tensor.transpose(nw_t[:], nw_rows[:], ident_bf[:])
             nc.vector.tensor_copy(out=nw_cols[:], in_=nw_t[:, 0 : 2 * H_BLOCKS])
-            spread_vec(0, bias_b)
-
-        def spread_vec(v, dst):
             bias_ps = psum_t.tile([P, H], BF16, tag="t")
             for hh in range(HALVES):
                 cols = slice(N_COLS * hh, N_COLS * (hh + 1))
-                nc.tensor.matmul(out=bias_ps[:, cols], lhsT=ones[:, 0:P], rhs=vec_rows[:, v, cols], start=True, stop=True)
-            nc.scalar.copy(out=dst[:], in_=bias_ps[:])
+                nc.tensor.matmul(out=bias_ps[:, cols], lhsT=ones[:, 0:P], rhs=bias_rows[:, cols], start=True, stop=True)
+            nc.scalar.copy(out=bias_b[:], in_=bias_ps[:])
 
         w_words = const.tile([P, PASSES, H], U32, align_bytes=64)
         w_scales = const.tile([P, PASSES, H], U8, align_bytes=64)
@@ -206,12 +202,20 @@ def tile_graphresblock_pa_kernel(tc, x, pre_w, pre_b, lin1_W, lin1_b, n1_w, n1_b
                 )
 
         def normalise(j, g):
-            xn[j, g] = xn_pool.tile([P, GROUP, PACK, P], F32, name="xn")
+            width = 1 if j < FINE else 2
+            if g % 2 == 0:
+                xn[j, g // 2] = xn_pool.tile([P, GROUP, 2 * PACK, P], F32, name="xn")
+            if g % width:
+                return
             for i in range(GROUP):
-                chunk = x_nat[GROUP * j + i][:, K_PASS * g : K_PASS * (g + 1)].rearrange("p (q t) -> p t q", t=PACK)
+                slots = slice(PACK * (g % 2), PACK * (g % 2 + width))
+                out_view = xn[j, g // 2][:, i, slots, :].rearrange("p (g t) q -> p g t q", t=PACK)
+                chunk = x_nat[GROUP * j + i][:, K_PASS * g : K_PASS * (g + width)].rearrange(
+                    "p (g q t) -> p g t q", q=P, t=PACK
+                )
                 if GROUP * j + i < SCALAR_NORM:
                     nc.scalar.activation(
-                        out=xn[j, g][:, i, :, :],
+                        out=out_view,
                         in_=chunk,
                         func=ACT.Identity,
                         scale=rstd[j][:, i : i + 1],
@@ -219,7 +223,7 @@ def tile_graphresblock_pa_kernel(tc, x, pre_w, pre_b, lin1_W, lin1_b, n1_w, n1_b
                     )
                 else:
                     nc.vector.tensor_scalar(
-                        out=xn[j, g][:, i, :, :],
+                        out=out_view,
                         in0=chunk,
                         scalar1=rstd[j][:, i : i + 1],
                         scalar2=shift[j][:, i : i + 1],
@@ -239,7 +243,7 @@ def tile_graphresblock_pa_kernel(tc, x, pre_w, pre_b, lin1_W, lin1_b, n1_w, n1_b
                 for s in range(2):
                     for i in range(GROUP):
                         nc.tensor.transpose(
-                            x_turned[b][:, s, P * i : P * i + P], xn[j, g][:, i, 2 * b + s, :], ident[:]
+                            x_turned[b][:, s, P * i : P * i + P], xn[j, g // 2][:, i, PACK * (g % 2) + 2 * b + s, :], ident[:]
                         )
 
         def gain_x(j, g):
@@ -452,8 +456,5 @@ def tile_graphresblock_pa_kernel(tc, x, pre_w, pre_b, lin1_W, lin1_b, n1_w, n1_b
             at(step, 6, 4, quantise_y)
             every_other(step, 12, spread_of)
             every_other(step, 12, gain_early)
-            if step == 18:
-                spread_vec(1, gain_b)
-                spread_vec(2, shift_b)
             if step == 8:
                 spread_post()

@@ -35,7 +35,9 @@ PIECES = (4, 2)
 FINE = 1
 SCALAR_NORM = 7
 
-STRAIGHT = 5
+IDLE_HEAD = 10
+
+STRAIGHT = 4
 
 FLOPS = 2 * TOKENS * C * H
 
@@ -353,7 +355,10 @@ def tile_graphresblock_pa_kernel(tc, x, pre_w, pre_b, lin1_W, lin1_b, n1_w, n1_b
                 n = GROUP * j + i
                 for hh in range(HALVES):
                     cols = slice(N_COLS * hh, N_COLS * (hh + 1))
-                    nc.vector.tensor_scalar_max(out=zn[j, i][:, cols], in0=zn[j, i][:, cols], scalar1=0.0)
+                    if hh == 0:
+                        nc.scalar.activation(out=zn[j, i][:, cols], in_=zn[j, i][:, cols], func=ACT.Relu)
+                    else:
+                        nc.vector.tensor_scalar_max(out=zn[j, i][:, cols], in0=zn[j, i][:, cols], scalar1=0.0)
                     nc.sync.dma_start(out=out_rows[P * n : P * n + P, cols], in_=zn[j, i][:, cols])
                 return
             zn[j, i] = z_pool.tile([P, H], F32, name="zn")
@@ -429,7 +434,7 @@ def tile_graphresblock_pa_kernel(tc, x, pre_w, pre_b, lin1_W, lin1_b, n1_w, n1_b
                 work(d // 4, d % 4 // 2)
 
         w_order = [(pair, g) for pair in range(W_TILES // 2) for g in range(PASSES)]
-        for r in range(4):
+        for r in range(IDLE_HEAD):
             warm(ones[:])
         spread_pre()
         for step in range(4 * GROUPS + 21):

@@ -161,6 +161,9 @@ def tile_graphresblock_pa_kernel(tc, x, pre_w, pre_b, lin1_W, lin1_b, n1_w, n1_b
                 out=w_words[:, g, cols].bitcast(FP8X4), scales=w_scales[:, g, cols], in_=w_grouped[pair, g][:]
             )
 
+        def width_of(j):
+            return 1 if j < FINE else 2
+
         stats = {}
         mean_var = {}
         rstd = {}
@@ -204,7 +207,7 @@ def tile_graphresblock_pa_kernel(tc, x, pre_w, pre_b, lin1_W, lin1_b, n1_w, n1_b
                 )
 
         def normalise(j, g):
-            width = 1 if j < FINE else 2
+            width = width_of(j)
             if g % 2 == 0:
                 xn[j, g // 2] = xn_pool.tile([P, GROUP, 2 * PACK, P], F32, name="xn")
             if g % width:
@@ -249,11 +252,12 @@ def tile_graphresblock_pa_kernel(tc, x, pre_w, pre_b, lin1_W, lin1_b, n1_w, n1_b
                         )
 
         def gain_x(j, g):
-            y_planes[j, g] = stage.tile([P, PACK, GROUP_TOKENS], BF16, name="y_planes")
+            if g % width_of(j) == 0:
+                y_planes[j, g // width_of(j)] = stage.tile([P, 2, PACK, GROUP_TOKENS], BF16, name="y_planes")
             for t in range(PACK):
                 c = PACK * g + t
                 nc.scalar.activation(
-                    out=y_planes[j, g][:, t, :],
+                    out=y_planes[j, g // width_of(j)][:, g % width_of(j), t, :],
                     in_=x_turned[t // 2][:, t % 2, :],
                     func=ACT.Relu,
                     scale=wb_cols[:, c : c + 1],
@@ -261,18 +265,29 @@ def tile_graphresblock_pa_kernel(tc, x, pre_w, pre_b, lin1_W, lin1_b, n1_w, n1_b
                 )
 
         def interleave_y(j, g):
-            y_grouped[j, g] = stage.tile([P, GROUP_TOKENS * PACK], BF16, align_bytes=64, name="y_grouped")
+            width = width_of(j)
+            if (g + 1) % width:
+                return
+            y_grouped[j, g // width_of(j)] = stage.tile([P, 2 * GROUP_TOKENS * PACK], BF16, align_bytes=64, name="y_grouped")
             nc.vector.tensor_copy(
-                out=y_grouped[j, g][:].rearrange("p (c i t) -> p c t i", i=4, t=PACK),
-                in_=y_planes[j, g][:].rearrange("p t (c i) -> p c t i", i=4),
+                out=y_grouped[j, g // width][:, 0 : width * PACK * GROUP_TOKENS].rearrange(
+                    "p (g c i t) -> p g c t i", g=width, i=4, t=PACK
+                ),
+                in_=y_planes[j, g // width][:, 0:width, :, :].rearrange("p g t (c i) -> p g c t i", i=4),
             )
 
         def quantise_y(j, g):
-            if g == 0:
+            width = width_of(j)
+            if (g + 1) % width:
+                return
+            if g == width - 1:
                 y_words[j] = y_pool.tile([P, PASSES, GROUP_TOKENS], U32, align_bytes=64, name="y_words")
                 y_scales[j] = y_pool.tile([P, PASSES, GROUP_TOKENS], U8, align_bytes=64, name="y_scales")
+            passes = slice(g + 1 - width, g + 1)
             nc.vector.quantize_mx(
-                out=y_words[j][:, g, :].bitcast(FP8X4), scales=y_scales[j][:, g, :], in_=y_grouped[j, g][:]
+                out=y_words[j][:, passes, :].rearrange("p g n -> p (g n)").bitcast(FP8X4),
+                scales=y_scales[j][:, passes, :].rearrange("p g n -> p (g n)"),
+                in_=y_grouped[j, g // width_of(j)][:, 0 : width * PACK * GROUP_TOKENS],
             )
 
         acc = {}
@@ -437,29 +452,29 @@ def tile_graphresblock_pa_kernel(tc, x, pre_w, pre_b, lin1_W, lin1_b, n1_w, n1_b
         for r in range(IDLE_HEAD):
             warm(ones[:])
         spread_pre()
-        for step in range(4 * GROUPS + 21):
+        for step in range(4 * GROUPS + 22):
             for pair, g in w_order[4 * step : 4 * step + 4]:
                 turn_w(pair, g)
             at(step, 4, 4, normalise)
-            every_other(step, 13, normalise_z)
+            every_other(step, 14, normalise_z)
             at(step, 5, 4, turn_x)
-            at(step, 16, 4, turn_z)
-            at(step, 18, 4, turn_back)
-            at(step, 10, 4, project)
+            at(step, 17, 4, turn_z)
+            at(step, 19, 4, turn_back)
+            at(step, 11, 4, project)
             at(step, 0, 4, measure)
-            at(step, 11, 4, add_bias)
+            at(step, 12, 4, add_bias)
             at(step, 5, 4, gain_x)
-            at(step, 16, 4, gain_z)
+            at(step, 17, 4, gain_z)
             at(step, 0, 4, aggregate)
             at(step, 0, 4, deviation)
+            at(step, 7, 4, quantise_y)
             at(step, 6, 4, interleave_y)
             for pair, g in w_order[4 * step : 4 * step + 4]:
                 quantise_w(pair, g)
                 warm_w(pair, g)
-            every_other(step, 12, centre)
-            at(step, 18, 4, store)
-            at(step, 6, 4, quantise_y)
-            every_other(step, 12, spread_of)
-            every_other(step, 12, gain_early)
+            every_other(step, 13, centre)
+            at(step, 19, 4, store)
+            every_other(step, 13, spread_of)
+            every_other(step, 13, gain_early)
             if step == 8:
                 spread_post()

@@ -32,12 +32,22 @@ BN_CHUNK = 512
 
 LOADS = "x0 w0 x1 w1 w2 w3 x2 x3 w4 w5 w6 w7"
 PIECES = (4, 2)
-FINE = 1
-SCALAR_NORM = 7
-
+ENGINES = {mybir.EngineType.DVE}
+NORM = "gggggggggggg"
+CT = 2
+JW = 2
+CQY = 3
+IL = "vvssvsvvvvvv"
+EARLY = True
+BACK = "ssssssssssss"
+WU = 4
+CQ = 1
+CI = 3
+CP = 5
+CA = 6
 IDLE_HEAD = 10
 
-STRAIGHT = 4
+PATH = "ttttttssttss"
 
 FLOPS = 2 * TOKENS * C * H
 
@@ -49,11 +59,11 @@ def tile_graphresblock_pa_kernel(tc, x, pre_w, pre_b, lin1_W, lin1_b, n1_w, n1_b
 
     with ExitStack() as stack:
         const = stack.enter_context(tc.tile_pool(name="const", bufs=1))
-        small = stack.enter_context(tc.tile_pool(name="small", bufs=4))
+        small = stack.enter_context(tc.tile_pool(name="small", bufs=6))
         rows_pool = stack.enter_context(tc.tile_pool(name="rows_pool", bufs=8))
-        xn_pool = stack.enter_context(tc.tile_pool(name="xn_pool", bufs=4))
-        stage = stack.enter_context(tc.tile_pool(name="stage", bufs=3))
-        y_pool = stack.enter_context(tc.tile_pool(name="y_pool", bufs=2))
+        xn_pool = stack.enter_context(tc.tile_pool(name="xn_pool", bufs=6))
+        stage = stack.enter_context(tc.tile_pool(name="stage", bufs=4))
+        y_pool = stack.enter_context(tc.tile_pool(name="y_pool", bufs=3))
         z_pool = stack.enter_context(tc.tile_pool(name="z_pool", bufs=4))
         out_pool = stack.enter_context(tc.tile_pool(name="out_pool", bufs=4))
         psum_t = stack.enter_context(tc.psum_pool(name="psum_t", bufs=5))
@@ -161,80 +171,60 @@ def tile_graphresblock_pa_kernel(tc, x, pre_w, pre_b, lin1_W, lin1_b, n1_w, n1_b
                 out=w_words[:, g, cols].bitcast(FP8X4), scales=w_scales[:, g, cols], in_=w_grouped[pair, g][:]
             )
 
-        def width_of(j):
-            return 1 if j < FINE else 2
-
         stats = {}
         mean_var = {}
+        std = {}
         rstd = {}
-        xn = {}
         shift = {}
+        xn = {}
 
-        def measure(j, k):
-            i = k // 2
-            if k == 0:
-                mean_var[j] = small.tile([P, GROUP, 2], F32, name="mean_var")
-                rstd[j] = small.tile([P, GROUP], F32, name="rstd")
-            if k % 2 == 0:
-                stats[j] = small.tile([P, C // BN_CHUNK, 6], F32, name="stats")
-            for s in (2 * (k % 2), 2 * (k % 2) + 1):
-                nc.vector.bn_stats(
-                    out=stats[j][:, s, :], in_=x_nat[GROUP * j + i][:, BN_CHUNK * s : BN_CHUNK * (s + 1)]
-                )
+        def measure(n, half):
+            if half == 0:
+                stats[n] = small.tile([P, C // BN_CHUNK, 6], F32, name="stats")
+            for s in (2 * half, 2 * half + 1):
+                nc.vector.bn_stats(out=stats[n][:, s, :], in_=x_nat[n][:, BN_CHUNK * s : BN_CHUNK * (s + 1)])
 
-        def aggregate(j, k):
-            i = k // 2
-            if k % 2 == 1:
-                nc.vector.bn_aggr(out=mean_var[j][:, i, :], in_=stats[j][:].rearrange("p s d -> p (s d)"))
+        def aggregate(n):
+            mean_var[n] = small.tile([P, 2], F32, name="mean_var")
+            nc.vector.bn_aggr(out=mean_var[n][:], in_=stats[n][:].rearrange("p s d -> p (s d)"))
 
-        def deviation(j, k):
-            if k == 1:
-                shift[j] = small.tile([P, GROUP], F32, name="shift")
-            if k == 3 or (k == 1 and j == 0):
-                sel = slice(k // 2, k // 2 + 1) if j == 0 else slice(0, GROUP)
-                std = small.tile([P, GROUP], F32, name="std")
+        def deviation(n):
+            std[n] = small.tile([P, 1], F32, name="std")
+            nc.scalar.activation(out=std[n][:], in_=mean_var[n][:, 1:2], func=ACT.Sqrt, bias=eps_col[:], scale=1.0)
+
+        def invert(n):
+            rstd[n] = small.tile([P, 1], F32, name="rstd")
+            nc.vector.reciprocal(out=rstd[n][:], in_=std[n][:])
+
+        def shift_x(n):
+            shift[n] = small.tile([P, 1], F32, name="shift")
+            nc.vector.tensor_scalar(
+                out=shift[n][:],
+                in0=mean_var[n][:, 0:1],
+                scalar1=rstd[n][:],
+                scalar2=-1.0,
+                op0=ALU.mult,
+                op1=ALU.mult,
+            )
+
+        def normalise(n, g, width):
+            j, i = n // GROUP, n % GROUP
+            if i == 0:
+                for h in range(g // 2, (g + width + 1) // 2):
+                    if 2 * h >= g:
+                        xn[j, h] = xn_pool.tile([P, GROUP, 2 * PACK, P], F32, name="xn")
+            out_view = xn[j, g // 2][:, i, PACK * (g % 2) : PACK * (g % 2 + width), :].rearrange(
+                "p (g t) q -> p g t q", t=PACK
+            )
+            chunk = x_nat[n][:, K_PASS * g : K_PASS * (g + width)].rearrange("p (g q t) -> p g t q", q=P, t=PACK)
+            if NORM[n] == "s":
                 nc.scalar.activation(
-                    out=std[:, sel], in_=mean_var[j][:, sel, 1], func=ACT.Sqrt, bias=eps_col[:], scale=1.0
+                    out=out_view, in_=chunk, func=ACT.Identity, scale=rstd[n][:], bias=shift[n][:]
                 )
-                nc.vector.reciprocal(out=rstd[j][:, sel], in_=std[:, sel])
-                nc.vector.scalar_tensor_tensor(
-                    out=shift[j][:, sel],
-                    in0=mean_var[j][:, sel, 0],
-                    scalar=-1.0,
-                    in1=rstd[j][:, sel],
-                    op0=ALU.mult,
-                    op1=ALU.mult,
+            else:
+                (nc.gpsimd if NORM[n] == "g" else nc.vector).tensor_scalar(
+                    out=out_view, in0=chunk, scalar1=rstd[n][:], scalar2=shift[n][:], op0=ALU.mult, op1=ALU.add
                 )
-
-        def normalise(j, g):
-            width = width_of(j)
-            if g % 2 == 0:
-                xn[j, g // 2] = xn_pool.tile([P, GROUP, 2 * PACK, P], F32, name="xn")
-            if g % width:
-                return
-            for i in range(GROUP):
-                slots = slice(PACK * (g % 2), PACK * (g % 2 + width))
-                out_view = xn[j, g // 2][:, i, slots, :].rearrange("p (g t) q -> p g t q", t=PACK)
-                chunk = x_nat[GROUP * j + i][:, K_PASS * g : K_PASS * (g + width)].rearrange(
-                    "p (g q t) -> p g t q", q=P, t=PACK
-                )
-                if GROUP * j + i < SCALAR_NORM:
-                    nc.scalar.activation(
-                        out=out_view,
-                        in_=chunk,
-                        func=ACT.Identity,
-                        scale=rstd[j][:, i : i + 1],
-                        bias=shift[j][:, i : i + 1],
-                    )
-                else:
-                    nc.vector.tensor_scalar(
-                        out=out_view,
-                        in0=chunk,
-                        scalar1=rstd[j][:, i : i + 1],
-                        scalar2=shift[j][:, i : i + 1],
-                        op0=ALU.mult,
-                        op1=ALU.add,
-                    )
 
         x_turned = {}
         y_planes = {}
@@ -252,42 +242,34 @@ def tile_graphresblock_pa_kernel(tc, x, pre_w, pre_b, lin1_W, lin1_b, n1_w, n1_b
                         )
 
         def gain_x(j, g):
-            if g % width_of(j) == 0:
-                y_planes[j, g // width_of(j)] = stage.tile([P, 2, PACK, GROUP_TOKENS], BF16, name="y_planes")
+            if g % JW == 0:
+                y_planes[j, g // JW] = stage.tile([P, JW, PACK, GROUP_TOKENS], BF16, name="y_planes")
             for t in range(PACK):
                 c = PACK * g + t
                 nc.scalar.activation(
-                    out=y_planes[j, g // width_of(j)][:, g % width_of(j), t, :],
+                    out=y_planes[j, g // JW][:, g % JW, t, :],
                     in_=x_turned[t // 2][:, t % 2, :],
                     func=ACT.Relu,
                     scale=wb_cols[:, c : c + 1],
                     bias=wb_cols[:, BLOCKS + c : BLOCKS + c + 1],
                 )
 
-        def interleave_y(j, g):
-            width = width_of(j)
-            if (g + 1) % width:
-                return
-            y_grouped[j, g // width_of(j)] = stage.tile([P, 2 * GROUP_TOKENS * PACK], BF16, align_bytes=64, name="y_grouped")
-            nc.vector.tensor_copy(
-                out=y_grouped[j, g // width][:, 0 : width * PACK * GROUP_TOKENS].rearrange(
-                    "p (g c i t) -> p g c t i", g=width, i=4, t=PACK
-                ),
-                in_=y_planes[j, g // width][:, 0:width, :, :].rearrange("p g t (c i) -> p g c t i", i=4),
+        def interleave_y(j, h):
+            y_grouped[j, h] = stage.tile([P, JW * GROUP_TOKENS * PACK], BF16, align_bytes=64, name="y_grouped")
+            (nc.scalar.copy if IL[2 * j + h] == "s" else nc.vector.tensor_copy)(
+                out=y_grouped[j, h][:].rearrange("p (g c i t) -> p g c t i", g=JW, i=4, t=PACK),
+                in_=y_planes[j, h][:].rearrange("p g t (c i) -> p g c t i", i=4),
             )
 
-        def quantise_y(j, g):
-            width = width_of(j)
-            if (g + 1) % width:
-                return
-            if g == width - 1:
+        def quantise_y(j, h):
+            if h == 0:
                 y_words[j] = y_pool.tile([P, PASSES, GROUP_TOKENS], U32, align_bytes=64, name="y_words")
                 y_scales[j] = y_pool.tile([P, PASSES, GROUP_TOKENS], U8, align_bytes=64, name="y_scales")
-            passes = slice(g + 1 - width, g + 1)
+            passes = slice(JW * h, JW * (h + 1))
             nc.vector.quantize_mx(
                 out=y_words[j][:, passes, :].rearrange("p g n -> p (g n)").bitcast(FP8X4),
                 scales=y_scales[j][:, passes, :].rearrange("p g n -> p (g n)"),
-                in_=y_grouped[j, g // width_of(j)][:, 0 : width * PACK * GROUP_TOKENS],
+                in_=y_grouped[j, h][:],
             )
 
         acc = {}
@@ -341,7 +323,7 @@ def tile_graphresblock_pa_kernel(tc, x, pre_w, pre_b, lin1_W, lin1_b, n1_w, n1_b
             )
 
         def gain_early(j, i):
-            if j >= STRAIGHT:
+            if PATH[GROUP * j + i] == "s":
                 zn[j, i] = z_pool.tile([P, H], F32, name="zn")
                 nc.vector.scalar_tensor_tensor(
                     out=zn[j, i][:], in0=z[j, i][:], scalar=neg_mean[j, i][:], in1=gain_b[:], op0=ALU.add, op1=ALU.mult
@@ -356,14 +338,20 @@ def tile_graphresblock_pa_kernel(tc, x, pre_w, pre_b, lin1_W, lin1_b, n1_w, n1_b
 
         zn = {}
 
-        def normalise_z(j, i):
-            std2 = small.tile([P, 1], F32, name="std2")
+        std2 = {}
+
+        def deviation_z(j, i):
+            std2[j, i] = small.tile([P, 1], F32, name="std2")
             nc.scalar.activation(
-                out=std2[:], in_=sum_sq[j, i][:], func=ACT.Sqrt, bias=eps_col[:], scale=1.0 / H
+                out=std2[j, i][:], in_=sum_sq[j, i][:], func=ACT.Sqrt, bias=eps_col[:], scale=1.0 / H
             )
+
+        def invert_z(j, i):
             rstd2[j, i] = small.tile([P, 1], F32, name="rstd2")
-            nc.vector.reciprocal(out=rstd2[j, i][:], in_=std2[:])
-            if j >= STRAIGHT:
+            nc.vector.reciprocal(out=rstd2[j, i][:], in_=std2[j, i][:])
+
+        def normalise_z(j, i):
+            if PATH[GROUP * j + i] == "s":
                 nc.vector.scalar_tensor_tensor(
                     out=zn[j, i][:], in0=zn[j, i][:], scalar=rstd2[j, i][:], in1=shift_b[:], op0=ALU.mult, op1=ALU.add
                 )
@@ -390,22 +378,27 @@ def tile_graphresblock_pa_kernel(tc, x, pre_w, pre_b, lin1_W, lin1_b, n1_w, n1_b
         res_t = {}
         res_back = {}
 
+        def turned_tiles(j):
+            return [i for i in range(GROUP) if PATH[GROUP * j + i] == "t"]
+
         def turn_z(j, k):
-            if j >= STRAIGHT:
+            tiles = turned_tiles(j)
+            if not tiles:
                 return
-            z_turned[j, k] = psum_t.tile([P, 2, GROUP_TOKENS], F32, name="zt", tag="t")
+            z_turned[j, k] = psum_t.tile([P, 2, P * len(tiles)], F32, name="zt", tag="t")
             for s in range(2):
                 hb = 2 * k + s
-                for i in range(GROUP):
+                for w, i in enumerate(tiles):
                     nc.tensor.transpose(
-                        z_turned[j, k][:, s, P * i : P * i + P], zn[j, i][:, P * hb : P * hb + P], ident[:]
+                        z_turned[j, k][:, s, P * w : P * w + P], zn[j, i][:, P * hb : P * hb + P], ident[:]
                     )
 
         def gain_z(j, k):
-            if j >= STRAIGHT:
+            tiles = turned_tiles(j)
+            if not tiles:
                 return
             if k == 0:
-                res_t[j] = out_pool.tile([P, H_BLOCKS, GROUP_TOKENS], F32, name="res_t", bufs=2)
+                res_t[j] = out_pool.tile([P, H_BLOCKS, P * len(tiles)], F32, name="res_t", bufs=2)
             for s in range(2):
                 hb = 2 * k + s
                 nc.scalar.activation(
@@ -417,64 +410,98 @@ def tile_graphresblock_pa_kernel(tc, x, pre_w, pre_b, lin1_W, lin1_b, n1_w, n1_b
                 )
 
         def turn_back(j, k):
-            if j >= STRAIGHT:
+            hh, w = k // 2, k % 2
+            if w >= len(turned_tiles(j)):
                 return
-            hh, i = k // 2, k % 2
             res_back[j, k] = psum_t.tile([P, N_COLS], F32, name="res_back", tag="t")
             for b in range(4):
                 nc.tensor.transpose(
-                    res_back[j, k][:, P * b : P * b + P], res_t[j][:, 4 * hh + b, P * i : P * i + P], ident[:]
+                    res_back[j, k][:, P * b : P * b + P], res_t[j][:, 4 * hh + b, P * w : P * w + P], ident[:]
                 )
 
         def store(j, k):
-            if j >= STRAIGHT:
+            hh, w = k // 2, k % 2
+            if w >= len(turned_tiles(j)):
                 return
-            hh, i = k // 2, k % 2
             res = out_pool.tile([P, N_COLS], F32, name="res")
-            if k == 0:
-                nc.vector.tensor_copy(out=res[:], in_=res_back[j, k][:])
-            else:
-                nc.scalar.copy(out=res[:], in_=res_back[j, k][:])
-            n = GROUP * j + i
+            (nc.vector.tensor_copy if BACK[GROUP * j + w] == "v" else nc.scalar.copy)(out=res[:], in_=res_back[j, k][:])
+            n = GROUP * j + turned_tiles(j)[w]
             nc.sync.dma_start(out=out_rows[P * n : P * n + P, N_COLS * hh : N_COLS * (hh + 1)], in_=res[:])
 
-        def at(step, lag, count, work):
-            d = step - lag
-            if d >= 0 and d // count < GROUPS:
-                work(d // count, d % count)
+        TILES = GROUP * GROUPS
 
-        def every_other(step, lag, work):
-            d = step - lag
-            if d >= 0 and d % 2 == 0 and d // 4 < GROUPS:
-                work(d // 4, d % 4 // 2)
+        def tile_at(c, lag, work, *more):
+            n = c - lag
+            if 0 <= n < TILES:
+                work(n, *more)
+
+        def units_at(c, lag, work):
+            for u in (2 * (c - lag), 2 * (c - lag) + 1):
+                if 0 <= u < 4 * GROUPS:
+                    work(u // 4, u % 4)
+
+        def pairs_at(c, lag, work):
+            for u in range((c - lag) * 2 // JW, (c - lag + 1) * 2 // JW):
+                if 0 <= u < 4 * GROUPS // JW:
+                    work(u * JW // 4, u % (4 // JW))
+
+        def second(work):
+            return lambda n: work(n // GROUP, n % GROUP)
 
         w_order = [(pair, g) for pair in range(W_TILES // 2) for g in range(PASSES)]
+
+        def w_at(c, work):
+            if c >= 0:
+                for pair, g in w_order[WU * c : WU * (c + 1)]:
+                    work(pair, g)
+
+        def v_norm(n):
+            return NORM[n] == "v"
+
         for r in range(IDLE_HEAD):
             warm(ones[:])
         spread_pre()
-        for step in range(4 * GROUPS + 22):
-            for pair, g in w_order[4 * step : 4 * step + 4]:
-                turn_w(pair, g)
-            at(step, 4, 4, normalise)
-            every_other(step, 14, normalise_z)
-            at(step, 5, 4, turn_x)
-            at(step, 17, 4, turn_z)
-            at(step, 19, 4, turn_back)
-            at(step, 11, 4, project)
-            at(step, 0, 4, measure)
-            at(step, 12, 4, add_bias)
-            at(step, 5, 4, gain_x)
-            at(step, 17, 4, gain_z)
-            at(step, 0, 4, aggregate)
-            at(step, 0, 4, deviation)
-            at(step, 7, 4, quantise_y)
-            at(step, 6, 4, interleave_y)
-            for pair, g in w_order[4 * step : 4 * step + 4]:
-                quantise_w(pair, g)
-                warm_w(pair, g)
-            every_other(step, 13, centre)
-            at(step, 19, 4, store)
-            every_other(step, 13, spread_of)
-            every_other(step, 13, gain_early)
-            if step == 8:
+        stack.enter_context(tc.manual_schedule(engines=ENGINES))
+        for c in range(TILES + CA + 6):
+            tile_at(c, CA + 1, second(deviation_z))
+            if EARLY:
+                tile_at(c, 1, shift_x)
+            tile_at(c, 0, measure, 0)
+            if not EARLY:
+                tile_at(c, 1, invert)
+            tile_at(c, 0, measure, 1)
+            if not EARLY:
+                tile_at(c, 1, shift_x)
+            for g in range(PASSES):
+                tile_at(c, 1, lambda n: None if v_norm(n) else normalise(n, g, 1))
+            tile_at(c, CA, lambda n: [add_bias(n // GROUP, 2 * (n % GROUP) + hh) for hh in range(2)])
+            tile_at(c, 0, aggregate)
+            tile_at(c, 0, deviation)
+            w_at(c, turn_w)
+            pairs_at(c, CI, interleave_y)
+            for g in (0, 2):
+                tile_at(c, 1, lambda n: normalise(n, g, 2) if v_norm(n) else None)
+            tile_at(c, CA, second(centre))
+            tile_at(c, CA, second(spread_of))
+            tile_at(c, CA + 1, second(invert_z))
+            pairs_at(c, CQY, quantise_y)
+            w_at(c - CQ, quantise_w)
+            w_at(c - CQ, warm_w)
+            tile_at(c, CA + 1, second(normalise_z))
+            tile_at(c, CA, second(gain_early))
+            if EARLY:
+                tile_at(c, 0, invert)
+            units_at(c, CT, lambda j, g: (turn_x(j, g), gain_x(j, g)))
+            tile_at(c, CP, lambda n: [project(n // GROUP, 2 * (n % GROUP) + hh) for hh in range(2)])
+            j = (c - CA - 2) // 2
+            if 0 <= j < GROUPS:
+                for k in (0, 1) if c % 2 == 0 else (2, 3):
+                    turn_z(j, k)
+                    gain_z(j, k)
+            j = (c - CA - 4) // 2
+            if 0 <= j < GROUPS:
+                for k in (0, 1) if c % 2 == 0 else (2, 3):
+                    turn_back(j, k)
+                    store(j, k)
+            if c == 4:
                 spread_post()

@@ -30,15 +30,25 @@ N_COLS = 512
 HALVES = H // N_COLS
 BN_CHUNK = 512
 
-LOADS = "x0 w0 x1 w1 w2 w3 x2 x3 w4 w5 w6 w7"
+LOADS = "x0 w0 x1 w1 w2 w3 x2 w4 w5 x3 w6 w7"
 PIECES = (4, 2)
 ENGINES = {mybir.EngineType.DVE}
 NORM = "gggggggggggg"
 CT = 2
+RB = 8
+CF = 7
+HP = 100
+POST = "s"
+DUMMY = (0, 0)
+ZN = "ggggvvvvvvvv"
+ZN_SPLIT = 1
 JW = 2
 CQY = 3
 IL = "vvssvsvvvvvv"
-EARLY = True
+AGG_FIRST = True
+INV_FIRST = True
+AHEAD = 2
+POST_C = 3
 BACK = "ssssssssssss"
 WU = 4
 CQ = 1
@@ -60,7 +70,7 @@ def tile_graphresblock_pa_kernel(tc, x, pre_w, pre_b, lin1_W, lin1_b, n1_w, n1_b
     with ExitStack() as stack:
         const = stack.enter_context(tc.tile_pool(name="const", bufs=1))
         small = stack.enter_context(tc.tile_pool(name="small", bufs=6))
-        rows_pool = stack.enter_context(tc.tile_pool(name="rows_pool", bufs=8))
+        rows_pool = stack.enter_context(tc.tile_pool(name="rows_pool", bufs=RB))
         xn_pool = stack.enter_context(tc.tile_pool(name="xn_pool", bufs=6))
         stage = stack.enter_context(tc.tile_pool(name="stage", bufs=4))
         y_pool = stack.enter_context(tc.tile_pool(name="y_pool", bufs=3))
@@ -94,14 +104,19 @@ def tile_graphresblock_pa_kernel(tc, x, pre_w, pre_b, lin1_W, lin1_b, n1_w, n1_b
                 cols = slice(C // pieces * s, C // pieces * (s + 1))
                 nc.sync.dma_start(out=x_nat[n][:, cols], in_=x_rows[P * n : P * n + P, cols])
 
-        def load_w(r):
-            w_nat[r] = rows_pool.tile([P, C], BF16, name="w_nat", tag="rows")
-            nc.sync.dma_start(out=w_nat[r][:], in_=lin1_W[P * r : P * r + P, :])
+        def load_w(r, piece=None):
+            if piece in (None, 0):
+                w_nat[r] = rows_pool.tile([P, C], BF16, name="w_nat", tag="rows")
+            cols = slice(0, C) if piece is None else slice(C // 2 * piece, C // 2 * (piece + 1))
+            nc.sync.dma_start(out=w_nat[r][:, cols], in_=lin1_W[P * r : P * r + P, cols])
 
         nc.sync.dma_start(out=wb_rows[0:PASSES, :], in_=pre_w.rearrange("(a c) -> a c", c=K_PASS))
         nc.sync.dma_start(out=wb_rows[PASSES : 2 * PASSES, :], in_=pre_b.rearrange("(a c) -> a c", c=K_PASS))
         for item in LOADS.split():
-            (load_x if item[0] == "x" else load_w)(int(item[1:]))
+            if item[0] == "x":
+                load_x(int(item[1:]))
+            else:
+                load_w(int(item[1]), {"a": 0, "b": 1}[item[2]] if len(item) > 2 else None)
         nc.sync.dma_start(out=bias_rows[0:1, :], in_=lin1_b.rearrange("(o h) -> o h", o=1))
         nc.sync.dma_start(out=nw_rows[0:H_BLOCKS, :], in_=n1_w.rearrange("(a c) -> a c", c=P))
         nc.sync.dma_start(out=nw_rows[H_BLOCKS : 2 * H_BLOCKS, :], in_=n1_b.rearrange("(a c) -> a c", c=P))
@@ -128,17 +143,23 @@ def tile_graphresblock_pa_kernel(tc, x, pre_w, pre_b, lin1_W, lin1_b, n1_w, n1_b
         nw_cols = const.tile([P, 2 * H_BLOCKS], F32)
         bias_b = const.tile([P, H], BF16)
 
-        def spread_post():
+        spread = {}
+
+        def turn_post():
             ident_bf = const.tile([P, P], BF16)
-            nc.vector.tensor_copy(out=ident_bf[:], in_=ident[:])
-            nw_t = psum_t.tile([P, P], BF16, tag="t")
-            nc.tensor.transpose(nw_t[:], nw_rows[:], ident_bf[:])
-            nc.vector.tensor_copy(out=nw_cols[:], in_=nw_t[:, 0 : 2 * H_BLOCKS])
-            bias_ps = psum_t.tile([P, H], BF16, tag="t")
+            nc.scalar.copy(out=ident_bf[:], in_=ident[:])
+            spread["nw"] = psum_t.tile([P, P], BF16, name="nw_t", tag="t")
+            nc.tensor.transpose(spread["nw"][:], nw_rows[:], ident_bf[:])
+            spread["bias"] = psum_t.tile([P, H], BF16, name="bias_ps", tag="t")
             for hh in range(HALVES):
                 cols = slice(N_COLS * hh, N_COLS * (hh + 1))
-                nc.tensor.matmul(out=bias_ps[:, cols], lhsT=ones[:, 0:P], rhs=bias_rows[:, cols], start=True, stop=True)
-            nc.scalar.copy(out=bias_b[:], in_=bias_ps[:])
+                nc.tensor.matmul(
+                    out=spread["bias"][:, cols], lhsT=ones[:, 0:P], rhs=bias_rows[:, cols], start=True, stop=True
+                )
+
+        def spread_post():
+            (nc.vector.tensor_copy if POST == "v" else nc.scalar.copy)(out=nw_cols[:], in_=spread["nw"][:, 0 : 2 * H_BLOCKS])
+            (nc.vector.tensor_copy if POST == "v" else nc.scalar.copy)(out=bias_b[:], in_=spread["bias"][:])
 
         w_words = const.tile([P, PASSES, H], U32, align_bytes=64)
         w_scales = const.tile([P, PASSES, H], U8, align_bytes=64)
@@ -235,6 +256,16 @@ def tile_graphresblock_pa_kernel(tc, x, pre_w, pre_b, lin1_W, lin1_b, n1_w, n1_b
         def turn_x(j, g):
             for b in range(2):
                 x_turned[b] = psum_t.tile([P, 2, GROUP_TOKENS], F32, name="xt", tag="t")
+                if DUMMY[b] and j > 0:
+                    nc.tensor.matmul_mx(
+                        out=x_turned[b][:].rearrange("p s n -> p (s n)"),
+                        lhsT=y_words[j - 1][:, 0, 0:P].bitcast(FP8X4),
+                        lhsT_scale=y_scales[j - 1][:, 0, 0:P],
+                        rhs=w_words[:, 0, 0:N_COLS].bitcast(FP8X4),
+                        rhs_scale=w_scales[:, 0, 0:N_COLS],
+                        start=True,
+                        stop=True,
+                    )
                 for s in range(2):
                     for i in range(GROUP):
                         nc.tensor.transpose(
@@ -355,24 +386,30 @@ def tile_graphresblock_pa_kernel(tc, x, pre_w, pre_b, lin1_W, lin1_b, n1_w, n1_b
                 nc.vector.scalar_tensor_tensor(
                     out=zn[j, i][:], in0=zn[j, i][:], scalar=rstd2[j, i][:], in1=shift_b[:], op0=ALU.mult, op1=ALU.add
                 )
-                n = GROUP * j + i
-                for hh in range(HALVES):
-                    cols = slice(N_COLS * hh, N_COLS * (hh + 1))
-                    if hh == 0:
-                        nc.scalar.activation(out=zn[j, i][:, cols], in_=zn[j, i][:, cols], func=ACT.Relu)
-                    else:
-                        nc.vector.tensor_scalar_max(out=zn[j, i][:, cols], in0=zn[j, i][:, cols], scalar1=0.0)
-                    nc.sync.dma_start(out=out_rows[P * n : P * n + P, cols], in_=zn[j, i][:, cols])
                 return
             zn[j, i] = z_pool.tile([P, H], F32, name="zn")
-            nc.vector.tensor_scalar(
-                out=zn[j, i][:],
-                in0=z[j, i][:],
-                scalar1=neg_mean[j, i][:],
-                scalar2=rstd2[j, i][:],
-                op0=ALU.add,
-                op1=ALU.mult,
-            )
+            for s in range(ZN_SPLIT):
+                cols = slice(H // ZN_SPLIT * s, H // ZN_SPLIT * (s + 1))
+                (nc.gpsimd if ZN[GROUP * j + i] == "g" else nc.vector).tensor_scalar(
+                    out=zn[j, i][:, cols],
+                    in0=z[j, i][:, cols],
+                    scalar1=neg_mean[j, i][:],
+                    scalar2=rstd2[j, i][:],
+                    op0=ALU.add,
+                    op1=ALU.mult,
+                )
+
+        def finish(j, i):
+            n = GROUP * j + i
+            if PATH[n] != "s":
+                return
+            for hh in range(HALVES):
+                cols = slice(N_COLS * hh, N_COLS * (hh + 1))
+                if hh == 0:
+                    nc.scalar.activation(out=zn[j, i][:, cols], in_=zn[j, i][:, cols], func=ACT.Relu)
+                else:
+                    nc.vector.tensor_scalar_max(out=zn[j, i][:, cols], in0=zn[j, i][:, cols], scalar1=0.0)
+                nc.sync.dma_start(out=out_rows[P * n : P * n + P, cols], in_=zn[j, i][:, cols])
 
         z_turned = {}
         res_t = {}
@@ -455,53 +492,78 @@ def tile_graphresblock_pa_kernel(tc, x, pre_w, pre_b, lin1_W, lin1_b, n1_w, n1_b
                 for pair, g in w_order[WU * c : WU * (c + 1)]:
                     work(pair, g)
 
-        def v_norm(n):
-            return NORM[n] == "v"
-
         for r in range(IDLE_HEAD):
             warm(ones[:])
         spread_pre()
         stack.enter_context(tc.manual_schedule(engines=ENGINES))
-        for c in range(TILES + CA + 6):
-            tile_at(c, CA + 1, second(deviation_z))
-            if EARLY:
+        def each_half(work):
+            return lambda n: [work(n // GROUP, 2 * (n % GROUP) + hh) for hh in range(2)]
+
+        def halves_at(c):
+            first = [(c, 0), (c, 1)]
+            second_ = []
+            if c >= AHEAD:
+                first = [(c, 1)]
+            if c + 1 >= AHEAD + 0 and c + 1 > 0 and c + 1 >= AHEAD:
+                second_ = [(c + 1, 0)]
+            return [[(n, h) for n, h in part if n < TILES] for part in (first, second_)]
+
+        for c in range(TILES + CF + 6):
+            with tc.high_priority(offset=HP):
+                tile_at(c, CA + 1, second(deviation_z))
+            before, after = halves_at(c)
+            if c != 1:
                 tile_at(c, 1, shift_x)
-            tile_at(c, 0, measure, 0)
-            if not EARLY:
-                tile_at(c, 1, invert)
-            tile_at(c, 0, measure, 1)
-            if not EARLY:
-                tile_at(c, 1, shift_x)
+            for n, h in before:
+                measure(n, h)
+                if c == 1 and h == 0:
+                    invert(0)
+            if c == 1:
+                shift_x(0)
             for g in range(PASSES):
-                tile_at(c, 1, lambda n: None if v_norm(n) else normalise(n, g, 1))
-            tile_at(c, CA, lambda n: [add_bias(n // GROUP, 2 * (n % GROUP) + hh) for hh in range(2)])
-            tile_at(c, 0, aggregate)
-            tile_at(c, 0, deviation)
-            w_at(c, turn_w)
+                tile_at(c, 1, normalise, g, 1)
+            tile_at(c, CA, each_half(add_bias))
+            if AGG_FIRST:
+                with tc.high_priority(offset=HP):
+                    tile_at(c, 0, aggregate)
+                    tile_at(c, 0, deviation)
+            for n, h in after:
+                measure(n, h)
             pairs_at(c, CI, interleave_y)
-            for g in (0, 2):
-                tile_at(c, 1, lambda n: normalise(n, g, 2) if v_norm(n) else None)
+            if not AGG_FIRST:
+                with tc.high_priority(offset=HP):
+                    tile_at(c, 0, aggregate)
+                    tile_at(c, 0, deviation)
+            w_at(c, turn_w)
+            tile_at(c, CF, second(invert_z))
             tile_at(c, CA, second(centre))
-            tile_at(c, CA, second(spread_of))
-            tile_at(c, CA + 1, second(invert_z))
+            with tc.high_priority(offset=HP):
+                tile_at(c, CA, second(spread_of))
+            if POST == "v" and c == POST_C + 1:
+                spread_post()
+            if INV_FIRST and c > 0:
+                tile_at(c, 0, invert)
             pairs_at(c, CQY, quantise_y)
             w_at(c - CQ, quantise_w)
             w_at(c - CQ, warm_w)
-            tile_at(c, CA + 1, second(normalise_z))
-            tile_at(c, CA, second(gain_early))
-            if EARLY:
+            if not INV_FIRST and c > 0:
                 tile_at(c, 0, invert)
+            tile_at(c, CF, second(normalise_z))
+            tile_at(c, CA, second(gain_early))
+            tile_at(c, CF, second(finish))
             units_at(c, CT, lambda j, g: (turn_x(j, g), gain_x(j, g)))
-            tile_at(c, CP, lambda n: [project(n // GROUP, 2 * (n % GROUP) + hh) for hh in range(2)])
-            j = (c - CA - 2) // 2
+            tile_at(c, CP, each_half(project))
+            j = (c - CF - 1) // 2
             if 0 <= j < GROUPS:
-                for k in (0, 1) if c % 2 == 0 else (2, 3):
+                for k in (0, 1) if (c - CF - 1) % 2 == 0 else (2, 3):
                     turn_z(j, k)
                     gain_z(j, k)
-            j = (c - CA - 4) // 2
+            j = (c - CF - 3) // 2
             if 0 <= j < GROUPS:
-                for k in (0, 1) if c % 2 == 0 else (2, 3):
+                for k in (0, 1) if (c - CF - 1) % 2 == 0 else (2, 3):
                     turn_back(j, k)
                     store(j, k)
-            if c == 4:
+            if c == POST_C:
+                turn_post()
+            if POST == "s" and c == POST_C:
                 spread_post()

@@ -40,7 +40,7 @@ CF = 7
 HP = 100
 POST = "s"
 DUMMY = (0, 0)
-ZN = "ggggvvvvvvvv"
+ZN = "vvvvvvvvvvvv"
 ZN_SPLIT = 1
 JW = 2
 CQY = 3

@@ -30,12 +30,16 @@ N_COLS = 512
 HALVES = H // N_COLS
 BN_CHUNK = 512
 
-LOADS = "x0 w0 x1 w1 w2 w3 x2 w4 w5 x3 w6 w7"
+LOADS = "x0 w0 x1 w1 w2 x2 w3 w4 w5 x3 w6 w7"
 PIECES = (4, 2)
 ENGINES = {mybir.EngineType.DVE}
-NORM = "gggggggggggg"
+NORM = "gggggggggggv"
 CT = 2
 RB = 8
+LATE_C = 99
+GW = 2
+GW_FROM = 1
+ADD_FIRST = False
 CF = 7
 HP = 100
 POST = "s"
@@ -71,7 +75,7 @@ def tile_graphresblock_pa_kernel(tc, x, pre_w, pre_b, lin1_W, lin1_b, n1_w, n1_b
         const = stack.enter_context(tc.tile_pool(name="const", bufs=1))
         small = stack.enter_context(tc.tile_pool(name="small", bufs=6))
         rows_pool = stack.enter_context(tc.tile_pool(name="rows_pool", bufs=RB))
-        xn_pool = stack.enter_context(tc.tile_pool(name="xn_pool", bufs=6))
+        xn_pool = stack.enter_context(tc.tile_pool(name="xn_pool", bufs=3))
         stage = stack.enter_context(tc.tile_pool(name="stage", bufs=4))
         y_pool = stack.enter_context(tc.tile_pool(name="y_pool", bufs=3))
         z_pool = stack.enter_context(tc.tile_pool(name="z_pool", bufs=4))
@@ -230,13 +234,9 @@ def tile_graphresblock_pa_kernel(tc, x, pre_w, pre_b, lin1_W, lin1_b, n1_w, n1_b
 
         def normalise(n, g, width):
             j, i = n // GROUP, n % GROUP
-            if i == 0:
-                for h in range(g // 2, (g + width + 1) // 2):
-                    if 2 * h >= g:
-                        xn[j, h] = xn_pool.tile([P, GROUP, 2 * PACK, P], F32, name="xn")
-            out_view = xn[j, g // 2][:, i, PACK * (g % 2) : PACK * (g % 2 + width), :].rearrange(
-                "p (g t) q -> p g t q", t=PACK
-            )
+            if g == 0 and i == 0:
+                xn[j] = xn_pool.tile([P, GROUP, PASSES * PACK, P], F32, name="xn")
+            out_view = xn[j][:, i, PACK * g : PACK * (g + width), :].rearrange("p (g t) q -> p g t q", t=PACK)
             chunk = x_nat[n][:, K_PASS * g : K_PASS * (g + width)].rearrange("p (g q t) -> p g t q", q=P, t=PACK)
             if NORM[n] == "s":
                 nc.scalar.activation(
@@ -269,7 +269,7 @@ def tile_graphresblock_pa_kernel(tc, x, pre_w, pre_b, lin1_W, lin1_b, n1_w, n1_b
                 for s in range(2):
                     for i in range(GROUP):
                         nc.tensor.transpose(
-                            x_turned[b][:, s, P * i : P * i + P], xn[j, g // 2][:, i, PACK * (g % 2) + 2 * b + s, :], ident[:]
+                            x_turned[b][:, s, P * i : P * i + P], xn[j][:, i, PACK * g + 2 * b + s, :], ident[:]
                         )
 
         def gain_x(j, g):
@@ -514,21 +514,25 @@ def tile_graphresblock_pa_kernel(tc, x, pre_w, pre_b, lin1_W, lin1_b, n1_w, n1_b
             before, after = halves_at(c)
             if c != 1:
                 tile_at(c, 1, shift_x)
+            if ADD_FIRST:
+                tile_at(c, CA, each_half(add_bias))
             for n, h in before:
                 measure(n, h)
                 if c == 1 and h == 0:
                     invert(0)
             if c == 1:
                 shift_x(0)
-            for g in range(PASSES):
-                tile_at(c, 1, normalise, g, 1)
-            tile_at(c, CA, each_half(add_bias))
+            for g in range(0, PASSES, GW if c > GW_FROM else 1):
+                tile_at(c, 1, normalise, g, GW if c > GW_FROM else 1)
+            if not ADD_FIRST:
+                tile_at(c, CA, each_half(add_bias))
             if AGG_FIRST:
                 with tc.high_priority(offset=HP):
                     tile_at(c, 0, aggregate)
                     tile_at(c, 0, deviation)
-            for n, h in after:
-                measure(n, h)
+            if c != LATE_C:
+                for n, h in after:
+                    measure(n, h)
             pairs_at(c, CI, interleave_y)
             if not AGG_FIRST:
                 with tc.high_priority(offset=HP):
@@ -546,6 +550,9 @@ def tile_graphresblock_pa_kernel(tc, x, pre_w, pre_b, lin1_W, lin1_b, n1_w, n1_b
             pairs_at(c, CQY, quantise_y)
             w_at(c - CQ, quantise_w)
             w_at(c - CQ, warm_w)
+            if c == LATE_C:
+                for n, h in after:
+                    measure(n, h)
             if not INV_FIRST and c > 0:
                 tile_at(c, 0, invert)
             tile_at(c, CF, second(normalise_z))

@@ -36,6 +36,12 @@ ENGINES = {mybir.EngineType.DVE}
 NORM = "gggggggggggv"
 CT = 2
 RB = 8
+RELU = "vvvvvvvvvvvv"
+ZB = 4
+RES = 8
+WB_AT = 1
+PRE = "v"
+PRE_C = -1
 LATE_C = 99
 GW = 2
 GW_FROM = 1
@@ -61,7 +67,7 @@ CP = 5
 CA = 6
 IDLE_HEAD = 10
 
-PATH = "ttttttssttss"
+PATH = "ttttttsstsss"
 
 FLOPS = 2 * TOKENS * C * H
 
@@ -114,9 +120,13 @@ def tile_graphresblock_pa_kernel(tc, x, pre_w, pre_b, lin1_W, lin1_b, n1_w, n1_b
             cols = slice(0, C) if piece is None else slice(C // 2 * piece, C // 2 * (piece + 1))
             nc.sync.dma_start(out=w_nat[r][:, cols], in_=lin1_W[P * r : P * r + P, cols])
 
-        nc.sync.dma_start(out=wb_rows[0:PASSES, :], in_=pre_w.rearrange("(a c) -> a c", c=K_PASS))
-        nc.sync.dma_start(out=wb_rows[PASSES : 2 * PASSES, :], in_=pre_b.rearrange("(a c) -> a c", c=K_PASS))
-        for item in LOADS.split():
+        def load_pre():
+            nc.sync.dma_start(out=wb_rows[0:PASSES, :], in_=pre_w.rearrange("(a c) -> a c", c=K_PASS))
+            nc.sync.dma_start(out=wb_rows[PASSES : 2 * PASSES, :], in_=pre_b.rearrange("(a c) -> a c", c=K_PASS))
+
+        for at_item, item in enumerate(LOADS.split()):
+            if at_item == WB_AT:
+                load_pre()
             if item[0] == "x":
                 load_x(int(item[1:]))
             else:
@@ -133,21 +143,24 @@ def tile_graphresblock_pa_kernel(tc, x, pre_w, pre_b, lin1_W, lin1_b, n1_w, n1_b
 
         wb_cols = const.tile([P, 2 * BLOCKS], F32)
 
-        def spread_pre():
-            wb_t = psum_t.tile([P, 2, P], F32, tag="t")
+        spread = {}
+
+        def turn_pre():
+            spread["wb"] = psum_t.tile([P, 2, P], F32, name="wb_t", tag="t")
             for u in range(2):
-                nc.tensor.transpose(wb_t[:, u, :], wb_rows[:].bitcast(F32)[:, u : 2 * P : 2], ident[:])
+                nc.tensor.transpose(spread["wb"][:, u, :], wb_rows[:].bitcast(F32)[:, u : 2 * P : 2], ident[:])
+
+        def spread_pre():
             wb_pairs = const.tile([P, 2 * BLOCKS], BF16)
-            nc.vector.tensor_copy(
+            copy = nc.scalar.copy if PRE == "s" else nc.vector.tensor_copy
+            copy(
                 out=wb_pairs[:].bitcast(F32).rearrange("p (a u) -> p a u", u=2),
-                in_=wb_t[:, :, 0 : 2 * PASSES].rearrange("p u a -> p a u"),
+                in_=spread["wb"][:, :, 0 : 2 * PASSES].rearrange("p u a -> p a u"),
             )
-            nc.vector.tensor_copy(out=wb_cols[:], in_=wb_pairs[:])
+            copy(out=wb_cols[:], in_=wb_pairs[:])
 
         nw_cols = const.tile([P, 2 * H_BLOCKS], F32)
         bias_b = const.tile([P, H], BF16)
-
-        spread = {}
 
         def turn_post():
             ident_bf = const.tile([P, P], BF16)
@@ -361,7 +374,7 @@ def tile_graphresblock_pa_kernel(tc, x, pre_w, pre_b, lin1_W, lin1_b, n1_w, n1_b
                 )
 
         def spread_of(j, i):
-            squares = stage.tile([P, H], BF16, name="squares")
+            squares = stage.tile([P, H], BF16, name="squares", bufs=2)
             sum_sq[j, i] = small.tile([P, 1], F32, name="sum_sq")
             nc.scalar.activation(
                 out=squares[:], in_=z[j, i][:], func=ACT.Square, bias=neg_mean[j, i][:], scale=1.0, accum_out=sum_sq[j, i][:]
@@ -405,7 +418,7 @@ def tile_graphresblock_pa_kernel(tc, x, pre_w, pre_b, lin1_W, lin1_b, n1_w, n1_b
                 return
             for hh in range(HALVES):
                 cols = slice(N_COLS * hh, N_COLS * (hh + 1))
-                if hh == 0:
+                if hh == 0 or RELU[n] == "s":
                     nc.scalar.activation(out=zn[j, i][:, cols], in_=zn[j, i][:, cols], func=ACT.Relu)
                 else:
                     nc.vector.tensor_scalar_max(out=zn[j, i][:, cols], in0=zn[j, i][:, cols], scalar1=0.0)
@@ -460,7 +473,7 @@ def tile_graphresblock_pa_kernel(tc, x, pre_w, pre_b, lin1_W, lin1_b, n1_w, n1_b
             hh, w = k // 2, k % 2
             if w >= len(turned_tiles(j)):
                 return
-            res = out_pool.tile([P, N_COLS], F32, name="res")
+            res = out_pool.tile([P, N_COLS], F32, name="res", bufs=RES)
             (nc.vector.tensor_copy if BACK[GROUP * j + w] == "v" else nc.scalar.copy)(out=res[:], in_=res_back[j, k][:])
             n = GROUP * j + turned_tiles(j)[w]
             nc.sync.dma_start(out=out_rows[P * n : P * n + P, N_COLS * hh : N_COLS * (hh + 1)], in_=res[:])
@@ -494,7 +507,9 @@ def tile_graphresblock_pa_kernel(tc, x, pre_w, pre_b, lin1_W, lin1_b, n1_w, n1_b
 
         for r in range(IDLE_HEAD):
             warm(ones[:])
-        spread_pre()
+        if PRE_C < 0:
+            turn_pre()
+            spread_pre()
         stack.enter_context(tc.manual_schedule(engines=ENGINES))
         def each_half(work):
             return lambda n: [work(n // GROUP, 2 * (n % GROUP) + hh) for hh in range(2)]
@@ -570,6 +585,9 @@ def tile_graphresblock_pa_kernel(tc, x, pre_w, pre_b, lin1_W, lin1_b, n1_w, n1_b
                 for k in (0, 1) if (c - CF - 1) % 2 == 0 else (2, 3):
                     turn_back(j, k)
                     store(j, k)
+            if c == PRE_C:
+                turn_pre()
+                spread_pre()
             if c == POST_C:
                 turn_post()
             if POST == "s" and c == POST_C:

from contextlib import ExitStack

import concourse.mybir as mybir
from concourse.masks import make_identity

F32 = mybir.dt.float32
BF16 = mybir.dt.bfloat16
I32 = mybir.dt.int32
U32 = mybir.dt.uint32
U8 = mybir.dt.uint8
FP8X4 = mybir.dt.float8_e4m3fn_x4
ACT = mybir.ActivationFunctionType
ALU = mybir.AluOpType

P = 128
TOKENS = 1536
C = 2048
H = 1024
EPS = 1e-12
PACK = 4
K_PASS = P * PACK
PASSES = C // K_PASS
BLOCKS = C // P
W_TILES = H // P
H_BLOCKS = H // P
GROUP = 2
GROUP_TOKENS = GROUP * P
GROUPS = TOKENS // GROUP_TOKENS
N_COLS = 512
HALVES = H // N_COLS
BN_CHUNK = 512

LOADS = "x0 w0 x1 w1 w2 x2 w3 w4 w5 x3 w6 w7"
PIECES = (4, 2)
ENGINES = {mybir.EngineType.DVE}
NORM = "gggggggggggv"
CT = 2
RB = 8
RELU = "vvvvvvvvvvvv"
ZB = 4
RES = 8
WB_AT = 1
PRE = "v"
PRE_C = -1
LATE_C = 99
GW = 2
GW_FROM = 1
ADD_FIRST = False
CF = 7
HP = 100
POST = "s"
DUMMY = (0, 0)
ZN = "vvvvvvvvvvvv"
ZN_SPLIT = 1
JW = 2
CQY = 3
IL = "vvssvsvvvvvv"
AGG_FIRST = True
INV_FIRST = True
AHEAD = 2
POST_C = 3
BACK = "ssssssssssss"
WU = 4
CQ = 1
CI = 3
CP = 5
CA = 6
IDLE_HEAD = 10

PATH = "ttttttsstsss"

FLOPS = 2 * TOKENS * C * H


def tile_graphresblock_pa_kernel(tc, x, pre_w, pre_b, lin1_W, lin1_b, n1_w, n1_b, out):
    nc = tc.nc
    x_rows = x.flatten_outer_dims()
    out_rows = out.flatten_outer_dims()

    with ExitStack() as stack:
        const = stack.enter_context(tc.tile_pool(name="const", bufs=1))
        small = stack.enter_context(tc.tile_pool(name="small", bufs=6))
        rows_pool = stack.enter_context(tc.tile_pool(name="rows_pool", bufs=RB))
        xn_pool = stack.enter_context(tc.tile_pool(name="xn_pool", bufs=3))
        stage = stack.enter_context(tc.tile_pool(name="stage", bufs=4))
        y_pool = stack.enter_context(tc.tile_pool(name="y_pool", bufs=3))
        z_pool = stack.enter_context(tc.tile_pool(name="z_pool", bufs=4))
        out_pool = stack.enter_context(tc.tile_pool(name="out_pool", bufs=4))
        psum_t = stack.enter_context(tc.psum_pool(name="psum_t", bufs=5))
        psum_acc = stack.enter_context(tc.psum_pool(name="psum_acc", bufs=3))

        ident = const.tile([P, P], F32)
        make_identity(nc, ident[:])
        ones = const.tile([P, N_COLS], BF16)
        nc.vector.memset(ones[:], 1.0)
        wb_rows = const.tile([P, K_PASS], BF16)
        nc.vector.memset(wb_rows[:].bitcast(I32), 0)
        eps_col = const.tile([P, 1], F32)
        nc.vector.memset(eps_col[:], EPS)
        table_warm = const.tile([P, 1], F32)
        nc.scalar.activation(out=table_warm[:], in_=eps_col[:], func=ACT.Sqrt)
        nw_rows = const.tile([P, P], BF16)
        nc.vector.memset(nw_rows[:].bitcast(I32), 0)
        bias_rows = const.tile([P, H], BF16)
        nc.vector.memset(bias_rows[:].bitcast(I32), 0)

        x_nat = {}
        w_nat = {}

        def load_x(n):
            x_nat[n] = rows_pool.tile([P, C], BF16, name="x_nat", tag="rows")
            pieces = PIECES[n] if n < len(PIECES) else 1
            for s in range(pieces):
                cols = slice(C // pieces * s, C // pieces * (s + 1))
                nc.sync.dma_start(out=x_nat[n][:, cols], in_=x_rows[P * n : P * n + P, cols])

        def load_w(r, piece=None):
            if piece in (None, 0):
                w_nat[r] = rows_pool.tile([P, C], BF16, name="w_nat", tag="rows")
            cols = slice(0, C) if piece is None else slice(C // 2 * piece, C // 2 * (piece + 1))
            nc.sync.dma_start(out=w_nat[r][:, cols], in_=lin1_W[P * r : P * r + P, cols])

        def load_pre():
            nc.sync.dma_start(out=wb_rows[0:PASSES, :], in_=pre_w.rearrange("(a c) -> a c", c=K_PASS))
            nc.sync.dma_start(out=wb_rows[PASSES : 2 * PASSES, :], in_=pre_b.rearrange("(a c) -> a c", c=K_PASS))

        for at_item, item in enumerate(LOADS.split()):
            if at_item == WB_AT:
                load_pre()
            if item[0] == "x":
                load_x(int(item[1:]))
            else:
                load_w(int(item[1]), {"a": 0, "b": 1}[item[2]] if len(item) > 2 else None)
        nc.sync.dma_start(out=bias_rows[0:1, :], in_=lin1_b.rearrange("(o h) -> o h", o=1))
        nc.sync.dma_start(out=nw_rows[0:H_BLOCKS, :], in_=n1_w.rearrange("(a c) -> a c", c=P))
        nc.sync.dma_start(out=nw_rows[H_BLOCKS : 2 * H_BLOCKS, :], in_=n1_b.rearrange("(a c) -> a c", c=P))
        for n in range(4, GROUP * GROUPS):
            load_x(n)
        gain_b = const.tile([P, H], BF16)
        nc.sync.dma_start(out=gain_b[:], in_=n1_w.partition_broadcast(P))
        shift_b = const.tile([P, H], BF16)
        nc.sync.dma_start(out=shift_b[:], in_=n1_b.partition_broadcast(P))

        wb_cols = const.tile([P, 2 * BLOCKS], F32)

        spread = {}

        def turn_pre():
            spread["wb"] = psum_t.tile([P, 2, P], F32, name="wb_t", tag="t")
            for u in range(2):
                nc.tensor.transpose(spread["wb"][:, u, :], wb_rows[:].bitcast(F32)[:, u : 2 * P : 2], ident[:])

        def spread_pre():
            wb_pairs = const.tile([P, 2 * BLOCKS], BF16)
            copy = nc.scalar.copy if PRE == "s" else nc.vector.tensor_copy
            copy(
                out=wb_pairs[:].bitcast(F32).rearrange("p (a u) -> p a u", u=2),
                in_=spread["wb"][:, :, 0 : 2 * PASSES].rearrange("p u a -> p a u"),
            )
            copy(out=wb_cols[:], in_=wb_pairs[:])

        nw_cols = const.tile([P, 2 * H_BLOCKS], F32)
        bias_b = const.tile([P, H], BF16)

        def turn_post():
            ident_bf = const.tile([P, P], BF16)
            nc.scalar.copy(out=ident_bf[:], in_=ident[:])
            spread["nw"] = psum_t.tile([P, P], BF16, name="nw_t", tag="t")
            nc.tensor.transpose(spread["nw"][:], nw_rows[:], ident_bf[:])
            spread["bias"] = psum_t.tile([P, H], BF16, name="bias_ps", tag="t")
            for hh in range(HALVES):
                cols = slice(N_COLS * hh, N_COLS * (hh + 1))
                nc.tensor.matmul(
                    out=spread["bias"][:, cols], lhsT=ones[:, 0:P], rhs=bias_rows[:, cols], start=True, stop=True
                )

        def spread_post():
            (nc.vector.tensor_copy if POST == "v" else nc.scalar.copy)(out=nw_cols[:], in_=spread["nw"][:, 0 : 2 * H_BLOCKS])
            (nc.vector.tensor_copy if POST == "v" else nc.scalar.copy)(out=bias_b[:], in_=spread["bias"][:])

        w_words = const.tile([P, PASSES, H], U32, align_bytes=64)
        w_scales = const.tile([P, PASSES, H], U8, align_bytes=64)
        w_grouped = {}

        warm_ps = psum_acc.tile([P, N_COLS], F32, name="warm_ps", tag="acc")

        def warm(src):
            nc.tensor.matmul(out=warm_ps[:], lhsT=ones[:, 0:P], rhs=src, start=True, stop=True)

        def turn_w(pair, g):
            wt = psum_t.tile([P, 2, 2 * P], F32, tag="t")
            for r in range(2):
                words = w_nat[2 * pair + r][:].bitcast(F32)
                for u in range(2):
                    first = 2 * P * g + u
                    nc.tensor.transpose(wt[:, u, P * r : P * r + P], words[:, first : 2 * P * (g + 1) : 2], ident[:])
            w_grouped[pair, g] = stage.tile([P, 2 * P * PACK], BF16, align_bytes=64, name="w_grouped")
            nc.scalar.copy(
                out=w_grouped[pair, g][:].bitcast(F32).rearrange("p (h u) -> p h u", u=2),
                in_=wt[:].rearrange("p u h -> p h u"),
            )

        def warm_w(pair, g):
            warm(w_grouped[pair, g][:, 0:N_COLS])

        def quantise_w(pair, g):
            cols = slice(2 * P * pair, 2 * P * (pair + 1))
            nc.vector.quantize_mx(
                out=w_words[:, g, cols].bitcast(FP8X4), scales=w_scales[:, g, cols], in_=w_grouped[pair, g][:]
            )

        stats = {}
        mean_var = {}
        std = {}
        rstd = {}
        shift = {}
        xn = {}

        def measure(n, half):
            if half == 0:
                stats[n] = small.tile([P, C // BN_CHUNK, 6], F32, name="stats")
            for s in (2 * half, 2 * half + 1):
                nc.vector.bn_stats(out=stats[n][:, s, :], in_=x_nat[n][:, BN_CHUNK * s : BN_CHUNK * (s + 1)])

        def aggregate(n):
            mean_var[n] = small.tile([P, 2], F32, name="mean_var")
            nc.vector.bn_aggr(out=mean_var[n][:], in_=stats[n][:].rearrange("p s d -> p (s d)"))

        def deviation(n):
            std[n] = small.tile([P, 1], F32, name="std")
            nc.scalar.activation(out=std[n][:], in_=mean_var[n][:, 1:2], func=ACT.Sqrt, bias=eps_col[:], scale=1.0)

        def invert(n):
            rstd[n] = small.tile([P, 1], F32, name="rstd")
            nc.vector.reciprocal(out=rstd[n][:], in_=std[n][:])

        def shift_x(n):
            shift[n] = small.tile([P, 1], F32, name="shift")
            nc.vector.tensor_scalar(
                out=shift[n][:],
                in0=mean_var[n][:, 0:1],
                scalar1=rstd[n][:],
                scalar2=-1.0,
                op0=ALU.mult,
                op1=ALU.mult,
            )

        def normalise(n, g, width):
            j, i = n // GROUP, n % GROUP
            if g == 0 and i == 0:
                xn[j] = xn_pool.tile([P, GROUP, PASSES * PACK, P], F32, name="xn")
            out_view = xn[j][:, i, PACK * g : PACK * (g + width), :].rearrange("p (g t) q -> p g t q", t=PACK)
            chunk = x_nat[n][:, K_PASS * g : K_PASS * (g + width)].rearrange("p (g q t) -> p g t q", q=P, t=PACK)
            if NORM[n] == "s":
                nc.scalar.activation(
                    out=out_view, in_=chunk, func=ACT.Identity, scale=rstd[n][:], bias=shift[n][:]
                )
            else:
                (nc.gpsimd if NORM[n] == "g" else nc.vector).tensor_scalar(
                    out=out_view, in0=chunk, scalar1=rstd[n][:], scalar2=shift[n][:], op0=ALU.mult, op1=ALU.add
                )

        x_turned = {}
        y_planes = {}
        y_grouped = {}
        y_words = {}
        y_scales = {}

        def turn_x(j, g):
            for b in range(2):
                x_turned[b] = psum_t.tile([P, 2, GROUP_TOKENS], F32, name="xt", tag="t")
                if DUMMY[b] and j > 0:
                    nc.tensor.matmul_mx(
                        out=x_turned[b][:].rearrange("p s n -> p (s n)"),
                        lhsT=y_words[j - 1][:, 0, 0:P].bitcast(FP8X4),
                        lhsT_scale=y_scales[j - 1][:, 0, 0:P],
                        rhs=w_words[:, 0, 0:N_COLS].bitcast(FP8X4),
                        rhs_scale=w_scales[:, 0, 0:N_COLS],
                        start=True,
                        stop=True,
                    )
                for s in range(2):
                    for i in range(GROUP):
                        nc.tensor.transpose(
                            x_turned[b][:, s, P * i : P * i + P], xn[j][:, i, PACK * g + 2 * b + s, :], ident[:]
                        )

        def gain_x(j, g):
            if g % JW == 0:
                y_planes[j, g // JW] = stage.tile([P, JW, PACK, GROUP_TOKENS], BF16, name="y_planes")
            for t in range(PACK):
                c = PACK * g + t
                nc.scalar.activation(
                    out=y_planes[j, g // JW][:, g % JW, t, :],
                    in_=x_turned[t // 2][:, t % 2, :],
                    func=ACT.Relu,
                    scale=wb_cols[:, c : c + 1],
                    bias=wb_cols[:, BLOCKS + c : BLOCKS + c + 1],
                )

        def interleave_y(j, h):
            y_grouped[j, h] = stage.tile([P, JW * GROUP_TOKENS * PACK], BF16, align_bytes=64, name="y_grouped")
            (nc.scalar.copy if IL[2 * j + h] == "s" else nc.vector.tensor_copy)(
                out=y_grouped[j, h][:].rearrange("p (g c i t) -> p g c t i", g=JW, i=4, t=PACK),
                in_=y_planes[j, h][:].rearrange("p g t (c i) -> p g c t i", i=4),
            )

        def quantise_y(j, h):
            if h == 0:
                y_words[j] = y_pool.tile([P, PASSES, GROUP_TOKENS], U32, align_bytes=64, name="y_words")
                y_scales[j] = y_pool.tile([P, PASSES, GROUP_TOKENS], U8, align_bytes=64, name="y_scales")
            passes = slice(JW * h, JW * (h + 1))
            nc.vector.quantize_mx(
                out=y_words[j][:, passes, :].rearrange("p g n -> p (g n)").bitcast(FP8X4),
                scales=y_scales[j][:, passes, :].rearrange("p g n -> p (g n)"),
                in_=y_grouped[j, h][:],
            )

        acc = {}
        z = {}
        z_sum = {}
        neg_mean = {}
        rstd2 = {}
        sum_sq = {}

        def project(j, k):
            i, hh = k // 2, k % 2
            tok = slice(P * i, P * i + P)
            cols = slice(N_COLS * hh, N_COLS * (hh + 1))
            acc[j, k] = psum_acc.tile([P, N_COLS], F32, name="acc", tag="acc")
            for g in range(PASSES):
                nc.tensor.matmul_mx(
                    out=acc[j, k][:],
                    lhsT=y_words[j][:, g, tok].bitcast(FP8X4),
                    lhsT_scale=y_scales[j][:, g, tok],
                    rhs=w_words[:, g, cols].bitcast(FP8X4),
                    rhs_scale=w_scales[:, g, cols],
                    start=(g == 0),
                    stop=(g == PASSES - 1),
                )

        def add_bias(j, k):
            i, hh = k // 2, k % 2
            cols = slice(N_COLS * hh, N_COLS * (hh + 1))
            if hh == 0:
                z[j, i] = z_pool.tile([P, H], F32, name="z")
                z_sum[j, i] = small.tile([P, HALVES], F32, name="z_sum")
            nc.vector.scalar_tensor_tensor(
                out=z[j, i][:, cols],
                in0=acc[j, k][:],
                scalar=1.0,
                in1=bias_b[:, cols],
                op0=ALU.mult,
                op1=ALU.add,
                accum_out=z_sum[j, i][:, hh : hh + 1],
            )

        def centre(j, i):
            neg_mean[j, i] = small.tile([P, 1], F32, name="neg_mean")
            nc.vector.tensor_scalar(
                out=neg_mean[j, i][:],
                in0=z_sum[j, i][:, 0:1],
                scalar1=z_sum[j, i][:, 1:2],
                scalar2=-1.0 / H,
                op0=ALU.add,
                op1=ALU.mult,
            )

        def gain_early(j, i):
            if PATH[GROUP * j + i] == "s":
                zn[j, i] = z_pool.tile([P, H], F32, name="zn")
                nc.vector.scalar_tensor_tensor(
                    out=zn[j, i][:], in0=z[j, i][:], scalar=neg_mean[j, i][:], in1=gain_b[:], op0=ALU.add, op1=ALU.mult
                )

        def spread_of(j, i):
            squares = stage.tile([P, H], BF16, name="squares", bufs=2)
            sum_sq[j, i] = small.tile([P, 1], F32, name="sum_sq")
            nc.scalar.activation(
                out=squares[:], in_=z[j, i][:], func=ACT.Square, bias=neg_mean[j, i][:], scale=1.0, accum_out=sum_sq[j, i][:]
            )

        zn = {}

        std2 = {}

        def deviation_z(j, i):
            std2[j, i] = small.tile([P, 1], F32, name="std2")
            nc.scalar.activation(
                out=std2[j, i][:], in_=sum_sq[j, i][:], func=ACT.Sqrt, bias=eps_col[:], scale=1.0 / H
            )

        def invert_z(j, i):
            rstd2[j, i] = small.tile([P, 1], F32, name="rstd2")
            nc.vector.reciprocal(out=rstd2[j, i][:], in_=std2[j, i][:])

        def normalise_z(j, i):
            if PATH[GROUP * j + i] == "s":
                nc.vector.scalar_tensor_tensor(
                    out=zn[j, i][:], in0=zn[j, i][:], scalar=rstd2[j, i][:], in1=shift_b[:], op0=ALU.mult, op1=ALU.add
                )
                return
            zn[j, i] = z_pool.tile([P, H], F32, name="zn")
            for s in range(ZN_SPLIT):
                cols = slice(H // ZN_SPLIT * s, H // ZN_SPLIT * (s + 1))
                (nc.gpsimd if ZN[GROUP * j + i] == "g" else nc.vector).tensor_scalar(
                    out=zn[j, i][:, cols],
                    in0=z[j, i][:, cols],
                    scalar1=neg_mean[j, i][:],
                    scalar2=rstd2[j, i][:],
                    op0=ALU.add,
                    op1=ALU.mult,
                )

        def finish(j, i):
            n = GROUP * j + i
            if PATH[n] != "s":
                return
            for hh in range(HALVES):
                cols = slice(N_COLS * hh, N_COLS * (hh + 1))
                if hh == 0 or RELU[n] == "s":
                    nc.scalar.activation(out=zn[j, i][:, cols], in_=zn[j, i][:, cols], func=ACT.Relu)
                else:
                    nc.vector.tensor_scalar_max(out=zn[j, i][:, cols], in0=zn[j, i][:, cols], scalar1=0.0)
                nc.sync.dma_start(out=out_rows[P * n : P * n + P, cols], in_=zn[j, i][:, cols])

        z_turned = {}
        res_t = {}
        res_back = {}

        def turned_tiles(j):
            return [i for i in range(GROUP) if PATH[GROUP * j + i] == "t"]

        def turn_z(j, k):
            tiles = turned_tiles(j)
            if not tiles:
                return
            z_turned[j, k] = psum_t.tile([P, 2, P * len(tiles)], F32, name="zt", tag="t")
            for s in range(2):
                hb = 2 * k + s
                for w, i in enumerate(tiles):
                    nc.tensor.transpose(
                        z_turned[j, k][:, s, P * w : P * w + P], zn[j, i][:, P * hb : P * hb + P], ident[:]
                    )

        def gain_z(j, k):
            tiles = turned_tiles(j)
            if not tiles:
                return
            if k == 0:
                res_t[j] = out_pool.tile([P, H_BLOCKS, P * len(tiles)], F32, name="res_t", bufs=2)
            for s in range(2):
                hb = 2 * k + s
                nc.scalar.activation(
                    out=res_t[j][:, hb, :],
                    in_=z_turned[j, k][:, s, :],
                    func=ACT.Relu,
                    scale=nw_cols[:, hb : hb + 1],
                    bias=nw_cols[:, H_BLOCKS + hb : H_BLOCKS + hb + 1],
                )

        def turn_back(j, k):
            hh, w = k // 2, k % 2
            if w >= len(turned_tiles(j)):
                return
            res_back[j, k] = psum_t.tile([P, N_COLS], F32, name="res_back", tag="t")
            for b in range(4):
                nc.tensor.transpose(
                    res_back[j, k][:, P * b : P * b + P], res_t[j][:, 4 * hh + b, P * w : P * w + P], ident[:]
                )

        def store(j, k):
            hh, w = k // 2, k % 2
            if w >= len(turned_tiles(j)):
                return
            res = out_pool.tile([P, N_COLS], F32, name="res", bufs=RES)
            (nc.vector.tensor_copy if BACK[GROUP * j + w] == "v" else nc.scalar.copy)(out=res[:], in_=res_back[j, k][:])
            n = GROUP * j + turned_tiles(j)[w]
            nc.sync.dma_start(out=out_rows[P * n : P * n + P, N_COLS * hh : N_COLS * (hh + 1)], in_=res[:])

        TILES = GROUP * GROUPS

        def tile_at(c, lag, work, *more):
            n = c - lag
            if 0 <= n < TILES:
                work(n, *more)

        def units_at(c, lag, work):
            for u in (2 * (c - lag), 2 * (c - lag) + 1):
                if 0 <= u < 4 * GROUPS:
                    work(u // 4, u % 4)

        def pairs_at(c, lag, work):
            for u in range((c - lag) * 2 // JW, (c - lag + 1) * 2 // JW):
                if 0 <= u < 4 * GROUPS // JW:
                    work(u * JW // 4, u % (4 // JW))

        def second(work):
            return lambda n: work(n // GROUP, n % GROUP)

        w_order = [(pair, g) for pair in range(W_TILES // 2) for g in range(PASSES)]

        def w_at(c, work):
            if c >= 0:
                for pair, g in w_order[WU * c : WU * (c + 1)]:
                    work(pair, g)

        for r in range(IDLE_HEAD):
            warm(ones[:])
        if PRE_C < 0:
            turn_pre()
            spread_pre()
        stack.enter_context(tc.manual_schedule(engines=ENGINES))
        def each_half(work):
            return lambda n: [work(n // GROUP, 2 * (n % GROUP) + hh) for hh in range(2)]

        def halves_at(c):
            first = [(c, 0), (c, 1)]
            second_ = []
            if c >= AHEAD:
                first = [(c, 1)]
            if c + 1 >= AHEAD + 0 and c + 1 > 0 and c + 1 >= AHEAD:
                second_ = [(c + 1, 0)]
            return [[(n, h) for n, h in part if n < TILES] for part in (first, second_)]

        for c in range(TILES + CF + 6):
            with tc.high_priority(offset=HP):
                tile_at(c, CA + 1, second(deviation_z))
            before, after = halves_at(c)
            if c != 1:
                tile_at(c, 1, shift_x)
            if ADD_FIRST:
                tile_at(c, CA, each_half(add_bias))
            for n, h in before:
                measure(n, h)
                if c == 1 and h == 0:
                    invert(0)
            if c == 1:
                shift_x(0)
            for g in range(0, PASSES, GW if c > GW_FROM else 1):
                tile_at(c, 1, normalise, g, GW if c > GW_FROM else 1)
            if not ADD_FIRST:
                tile_at(c, CA, each_half(add_bias))
            if AGG_FIRST:
                with tc.high_priority(offset=HP):
                    tile_at(c, 0, aggregate)
                    tile_at(c, 0, deviation)
            if c != LATE_C:
                for n, h in after:
                    measure(n, h)
            pairs_at(c, CI, interleave_y)
            if not AGG_FIRST:
                with tc.high_priority(offset=HP):
                    tile_at(c, 0, aggregate)
                    tile_at(c, 0, deviation)
            w_at(c, turn_w)
            tile_at(c, CF, second(invert_z))
            tile_at(c, CA, second(centre))
            with tc.high_priority(offset=HP):
                tile_at(c, CA, second(spread_of))
            if POST == "v" and c == POST_C + 1:
                spread_post()
            if INV_FIRST and c > 0:
                tile_at(c, 0, invert)
            pairs_at(c, CQY, quantise_y)
            w_at(c - CQ, quantise_w)
            w_at(c - CQ, warm_w)
            if c == LATE_C:
                for n, h in after:
                    measure(n, h)
            if not INV_FIRST and c > 0:
                tile_at(c, 0, invert)
            tile_at(c, CF, second(normalise_z))
            tile_at(c, CA, second(gain_early))
            tile_at(c, CF, second(finish))
            units_at(c, CT, lambda j, g: (turn_x(j, g), gain_x(j, g)))
            tile_at(c, CP, each_half(project))
            j = (c - CF - 1) // 2
            if 0 <= j < GROUPS:
                for k in (0, 1) if (c - CF - 1) % 2 == 0 else (2, 3):
                    turn_z(j, k)
                    gain_z(j, k)
            j = (c - CF - 3) // 2
            if 0 <= j < GROUPS:
                for k in (0, 1) if (c - CF - 1) % 2 == 0 else (2, 3):
                    turn_back(j, k)
                    store(j, k)
            if c == PRE_C:
                turn_pre()
                spread_pre()
            if c == POST_C:
                turn_post()
            if POST == "s" and c == POST_C:
                spread_post()
